import numpy as np
import ml_dtypes


def mxq(x, axis, fmt="e4m3"):
    dtype, down = {"e4m3": (ml_dtypes.float8_e4m3fn, 7), "e5m2": (ml_dtypes.float8_e5m2, 14)}[fmt]
    v = np.moveaxis(np.asarray(x, np.float32).astype(ml_dtypes.bfloat16).astype(np.float64), axis, -1)
    blocks = v.reshape(v.shape[:-1] + (-1, 32))
    amax = np.abs(blocks).max(-1, keepdims=True)
    byte = np.maximum(np.where(amax > 0, np.frexp(amax)[1] - 1 + 127, 0) - down, 1)
    scale = np.exp2(byte - 127.0)
    codes = (blocks / scale).astype(np.float32).astype(dtype).astype(np.float64)
    return np.moveaxis((codes * scale).reshape(v.shape), -1, axis)


WIDE = False


def mx_kscale(k):
    if not WIDE:
        return np.ones(k)
    levels = np.array([10, -10, 5, -5, 0])
    a = np.random.permutation(np.resize(levels, k // 512 * 4)).reshape(k // 512, 4)
    idx = np.arange(k)
    return np.exp2(a[idx // 512, idx % 128 // 32])


BF16 = ml_dtypes.bfloat16


def bf(x):
    return np.asarray(x, np.float32).astype(BF16)


def f64(x):
    return np.asarray(x).astype(np.float64)


E2M1 = np.array([0.0, 0.5, 1.0, 1.5, 2.0, 3.0, 4.0, 6.0, -0.0, -0.5, -1.0, -1.5, -2.0, -3.0, -4.0, -6.0])


def pack_weight(w, fmt):
    k, n = w.shape
    w = f64(bf(w)).reshape(k // 32, 32, n)
    amax = np.abs(w).max(1)
    if fmt == "e4m3":
        byte = np.frexp(amax)[1] - 1 + 127 - 7
    else:
        mant, ex = np.frexp(amax / 6.0)
        byte = np.where(mant > 0.5, ex, ex - 1) + 127
    byte = np.clip(np.where(amax > 0, byte, 1), 1, 254)
    scaled = (w * np.exp2(127.0 - byte)[:, None, :]).reshape(k, n).astype(np.float32)
    by_word = np.ascontiguousarray(scaled.reshape(k // 512, 128, 4, n).transpose(0, 1, 3, 2))
    if fmt == "e4m3":
        words = by_word.astype(ml_dtypes.float8_e4m3fn).view(np.uint8)
    else:
        c = by_word.astype(ml_dtypes.float4_e2m1fn).view(np.uint8) & 0xF
        words = c[..., 0::2] | (c[..., 1::2] << 4)
    return np.ascontiguousarray(words), np.ascontiguousarray(byte.astype(np.uint8).reshape(k // 512, 16, n))


def unpack_weight(words, scales, fmt):
    g, p, n, _ = words.shape
    if fmt == "e4m3":
        vals = np.ascontiguousarray(words).view(ml_dtypes.float8_e4m3fn).astype(np.float64)
    else:
        nib = np.empty((g, p, n, 4), np.uint8)
        nib[..., 0::2] = words & 0xF
        nib[..., 1::2] = words >> 4
        vals = E2M1[nib]
    vals = vals * np.repeat(np.exp2(scales.astype(np.float64) - 127.0), 8, axis=1)[..., None]
    return vals.transpose(0, 1, 3, 2).reshape(g * 512, n)


B, I, H = 512, 1024, 1024
EPS = 1e-5
FMT = "e4m3"
assert I % 512 == 0 and H % 512 == 0


def sigmoid(v):
    return 1.0 / (1.0 + np.exp(-v))


def setup_inputs():
    s = mx_kscale(I)
    t = mx_kscale(H)
    x = bf(np.random.standard_normal((B, I)) * s)
    h = bf(np.random.standard_normal((B, H)) * t)
    c = bf(np.random.standard_normal((B, H)))
    W_ih_words, W_ih_scales = pack_weight(np.ascontiguousarray((np.random.uniform(-1.0, 1.0, (4 * H, I)) / np.sqrt(I) / s[None, :]).T), FMT)
    b_ih = bf(np.random.standard_normal(4 * H) * 0.1)
    W_hh_words, W_hh_scales = pack_weight(np.ascontiguousarray((np.random.uniform(-1.0, 1.0, (4 * H, H)) / np.sqrt(H) / t[None, :]).T), FMT)
    b_hh = bf(np.random.standard_normal(4 * H) * 0.1)
    ln_w = bf(1.0 + np.random.standard_normal(H) * 0.1)
    ln_b = bf(np.random.standard_normal(H) * 0.1)
    return {"x": x,
            "h": h,
            "c": c,
            "W_ih_words": W_ih_words,
            "W_ih_scales": W_ih_scales,
            "b_ih": b_ih,
            "W_hh_words": W_hh_words,
            "W_hh_scales": W_hh_scales,
            "b_hh": b_hh,
            "ln_w": ln_w,
            "ln_b": ln_b}


def reference(x, h, c, W_ih_words, W_ih_scales, b_ih, W_hh_words, W_hh_scales, b_hh, ln_w, ln_b):
    xw = mxq(f64(x), 1, "e4m3") @ unpack_weight(W_ih_words, W_ih_scales, FMT)
    hw = mxq(f64(h), 1, "e4m3") @ unpack_weight(W_hh_words, W_hh_scales, FMT)
    preact = xw + f64(b_ih) + hw + f64(b_hh)
    gates = sigmoid(preact[:, :3 * H])
    g_t = np.tanh(preact[:, 3 * H:])
    i_t = gates[:, :H]
    f_t = gates[:, H:2 * H]
    o_t = gates[:, 2 * H:3 * H]
    c_t = f64(c) * f_t + i_t * g_t
    mu = np.mean(c_t, axis=-1, keepdims=True)
    var = np.mean(np.square(c_t - mu), axis=-1, keepdims=True)
    c_t = (c_t - mu) / np.sqrt(var + EPS) * f64(ln_w) + f64(ln_b)
    h_t = o_t * np.tanh(c_t)
    return (h_t, c_t)

@@ -1,0 +1,250 @@
+from contextlib import ExitStack
+
+import concourse.mybir as mybir
+from concourse.masks import make_identity
+
+F32 = mybir.dt.float32
+BF16 = mybir.dt.bfloat16
+I32 = mybir.dt.int32
+U32 = mybir.dt.uint32
+U8 = mybir.dt.uint8
+FP8X4 = mybir.dt.float8_e4m3fn_x4
+ALU = mybir.AluOpType
+ACT = mybir.ActivationFunctionType
+
+P = 128
+PACK = 4
+BATCH = 512
+HIDDEN = 1024
+BATCH_TILES = BATCH // P
+GROUPS = HIDDEN // (P * PACK)
+K_GROUPS = 2 * GROUPS
+CHUNK = 512
+HALVES = HIDDEN // CHUNK
+EPS = 1e-5
+
+GATE_I, GATE_F, GATE_O, GATE_G = 0, 1, 2, 3
+
+CELL_GATES = (GATE_I, GATE_G, GATE_F)
+
+PHASES = ((0, 1), (2,), (3,))
+
+FLOPS = 2 * BATCH * (2 * HIDDEN) * (4 * HIDDEN)
+
+
+def tile_lstmcelllayernorm_kernel(
+    tc, x, h, c, W_ih_words, W_ih_scales, b_ih, W_hh_words, W_hh_scales, b_hh, ln_w, ln_b, out_0, out_1
+):
+    nc = tc.nc
+    with ExitStack() as stack:
+        keep = stack.enter_context(tc.tile_pool(name="keep", bufs=1))
+        stage = stack.enter_context(tc.tile_pool(name="stage", bufs=2))
+        gates = stack.enter_context(tc.tile_pool(name="gates", bufs=4))
+        work = stack.enter_context(tc.tile_pool(name="work", bufs=2))
+        stats = stack.enter_context(tc.tile_pool(name="stats", bufs=4))
+        psum_acc = stack.enter_context(tc.psum_pool(name="psum_acc", bufs=6))
+        psum_flip = stack.enter_context(tc.psum_pool(name="psum_flip", bufs=2))
+
+        warm = keep.tile([P, 1], F32, name="warm")
+        nc.vector.memset(warm[:], 0.0)
+        nc.scalar.activation(out=warm[:], in_=warm[:], func=ACT.Sigmoid)
+
+        ident = keep.tile([P, P], F32, name="ident")
+        make_identity(nc, ident[:])
+        ones = keep.tile([P, P], BF16, name="ones")
+        nc.vector.memset(ones[:], 1.0)
+        neg_half = keep.tile([P, 1], F32, name="neg_half")
+        nc.gpsimd.memset(neg_half[:], -0.5)
+
+        x_sb = keep.tile([P, BATCH_TILES, HIDDEN], BF16, name="x_sb")
+        h_sb = keep.tile([P, BATCH_TILES, HIDDEN], BF16, name="h_sb")
+        c_sb = keep.tile([P, BATCH_TILES, HIDDEN], BF16, name="c_sb")
+
+        def load_batch_tile(dst, src, m):
+            nc.sync.dma_start(out=dst[:, m, :], in_=src[m * P : (m + 1) * P, :])
+
+        w_words = keep.tile([P, K_GROUPS, 4 * HIDDEN], U32, name="w_words", align_bytes=64)
+
+        def load_weight_chunk(gate, half):
+            col0 = gate * HIDDEN + half * CHUNK
+            for w, words in enumerate((W_ih_words, W_hh_words)):
+                by_partition = words.rearrange("g p n t -> p g (n t)")
+                nc.sync.dma_start(
+                    out=w_words[:, GROUPS * w : GROUPS * (w + 1), col0 : col0 + CHUNK].bitcast(I32),
+                    in_=by_partition[:, :, PACK * col0 : PACK * (col0 + CHUNK)].bitcast(I32),
+                )
+
+        w_scales = keep.tile([P, 4 * HIDDEN], U8, name="w_scales", align_bytes=64)
+        nc.vector.memset(w_scales[:].bitcast(I32), 0)
+
+        def load_weight_scales():
+            for quadrant in range(4):
+                for w, scales in enumerate((W_ih_scales, W_hh_scales)):
+                    first = 32 * quadrant + 4 * GROUPS * w
+                    nc.sync.dma_start(
+                        out=w_scales[first : first + 4 * GROUPS, :].bitcast(I32),
+                        in_=scales[:, 4 * quadrant : 4 * quadrant + 4, :].bitcast(I32),
+                    )
+
+        VECTOR_COLS = 4 * HIDDEN + 2 * HIDDEN
+        LN_W0 = 4 * HIDDEN
+        LN_B0 = 5 * HIDDEN
+        rows = keep.tile([P, VECTOR_COLS], BF16, name="rows")
+        nc.vector.memset(rows[:], 0.0)
+        nc.scalar.dma_start(out=rows[0:1, 0 : 4 * HIDDEN], in_=b_ih.unsqueeze(0))
+        nc.scalar.dma_start(out=rows[1:2, 0 : 4 * HIDDEN], in_=b_hh.unsqueeze(0))
+        nc.scalar.dma_start(out=rows[0:1, LN_W0 : LN_W0 + HIDDEN], in_=ln_w.unsqueeze(0))
+        nc.scalar.dma_start(out=rows[0:1, LN_B0 : LN_B0 + HIDDEN], in_=ln_b.unsqueeze(0))
+
+        for m in PHASES[0]:
+            load_batch_tile(x_sb, x, m)
+            load_batch_tile(h_sb, h, m)
+        load_weight_scales()
+        for gate in CELL_GATES:
+            load_weight_chunk(gate, 0)
+        for m in range(BATCH_TILES):
+            load_batch_tile(c_sb, c, m)
+        for tiles in PHASES[1:]:
+            for m in tiles:
+                load_batch_tile(x_sb, x, m)
+                load_batch_tile(h_sb, h, m)
+        for gate in CELL_GATES:
+            load_weight_chunk(gate, 1)
+        for half in range(HALVES):
+            load_weight_chunk(GATE_O, half)
+
+        xh_codes = keep.tile([P, BATCH_TILES, K_GROUPS * P], U32, name="xh_codes", align_bytes=64)
+        xh_scales = keep.tile([P, BATCH_TILES, K_GROUPS * P], U8, name="xh_scales", align_bytes=64)
+
+        def quantise_batch_tile(m):
+            grouped = stage.tile([P, K_GROUPS, P, PACK], BF16, name="grouped", align_bytes=64)
+            grouped_words = grouped[:].bitcast(F32)
+            for w, src in enumerate((x_sb, h_sb)):
+                words = src[:, m, :].bitcast(F32)
+                per_group = HIDDEN // 2 // GROUPS
+                flipped = psum_flip.tile([P, GROUPS, 2, P], F32, name="flipped")
+                for g in range(GROUPS):
+                    for u in range(2):
+                        nc.tensor.transpose(
+                            flipped[:, g, u, :],
+                            words[:, per_group * g + u : per_group * (g + 1) : 2],
+                            ident[:],
+                        )
+                dst = grouped_words[:, GROUPS * w : GROUPS * (w + 1), :, :]
+                pairs = flipped[:].rearrange("p g u r -> p g r u")
+                nc.scalar.copy(out=dst, in_=pairs)
+            nc.vector.quantize_mx(
+                out=xh_codes[:, m, :].bitcast(FP8X4),
+                scales=xh_scales[:, m, :],
+                in_=grouped[:].rearrange("p g r t -> p (g r t)"),
+            )
+
+        for m in PHASES[0]:
+            quantise_batch_tile(m)
+
+        spread = keep.tile([P, VECTOR_COLS], F32, name="spread")
+        spread_order = [gate * HIDDEN + half * CHUNK for half in range(HALVES) for gate in CELL_GATES]
+        spread_order += [first + half * CHUNK for first in (LN_W0, LN_B0, GATE_O * HIDDEN) for half in range(HALVES)]
+        for position, col0 in enumerate(spread_order):
+            summed = psum_acc.tile([P, CHUNK], F32, name="acc")
+            nc.tensor.matmul(out=summed[:], lhsT=ones[:], rhs=rows[:, col0 : col0 + CHUNK], start=True, stop=True)
+            if position % 2 == 0:
+                nc.vector.tensor_copy(out=spread[:, col0 : col0 + CHUNK], in_=summed[:])
+            else:
+                nc.scalar.copy(out=spread[:, col0 : col0 + CHUNK], in_=summed[:])
+
+        def gate_chunk(m, gate, half):
+            col0 = gate * HIDDEN + half * CHUNK
+            acc = psum_acc.tile([P, CHUNK], F32, name="acc")
+            for kg in range(K_GROUPS):
+                nc.tensor.matmul_mx(
+                    out=acc[:],
+                    lhsT=xh_codes[:, m, kg * P : (kg + 1) * P].bitcast(FP8X4),
+                    lhsT_scale=xh_scales[:, m, kg * P : (kg + 1) * P],
+                    rhs=w_words[:, kg, col0 : col0 + CHUNK].bitcast(FP8X4),
+                    rhs_scale=w_scales[4 * kg : P, col0 : col0 + CHUNK],
+                    start=(kg == 0),
+                    stop=(kg == K_GROUPS - 1),
+                )
+            gate_name = "gate%d" % gate
+            value = gates.tile([P, CHUNK], F32, name=gate_name)
+            nc.vector.tensor_tensor(out=value[:], in0=acc[:], in1=spread[:, col0 : col0 + CHUNK], op=ALU.add)
+            nc.scalar.activation(out=value[:], in_=value[:], func=(ACT.Tanh if gate == GATE_G else ACT.Sigmoid))
+            return value
+
+        def layer_norm(m, u, u_sum):
+            batch_rows = slice(m * P, (m + 1) * P)
+            neg_mean = stats.tile([P, 1], F32, name="neg_mean")
+            nc.vector.tensor_scalar(
+                out=neg_mean[:], in0=u_sum[:, 0:1], scalar1=u_sum[:, 1:2], scalar2=-1.0 / HIDDEN,
+                op0=ALU.add, op1=ALU.mult,
+            )
+            neg_mean_scaled = stats.tile([P, 1], F32, name="neg_mean_scaled")
+            nc.vector.tensor_scalar(
+                out=neg_mean_scaled[:], in0=neg_mean[:], scalar1=HIDDEN**-0.5, scalar2=None, op0=ALU.mult
+            )
+            squares = work.tile([P, HIDDEN], BF16, name="squares")
+            var = stats.tile([P, 1], F32, name="var")
+            nc.scalar.activation(
+                out=squares[:], in_=u[:], func=ACT.Square, bias=neg_mean_scaled[:], scale=HIDDEN**-0.5,
+                accum_out=var[:],
+            )
+            c_t = work.tile([P, HIDDEN], F32, name="c_t")
+            nc.vector.scalar_tensor_tensor(
+                out=c_t[:], in0=u[:], scalar=neg_mean[:], in1=spread[:, LN_W0 : LN_W0 + HIDDEN],
+                op0=ALU.add, op1=ALU.mult,
+            )
+            var_eps = stats.tile([P, 1], F32, name="var_eps")
+            nc.gpsimd.tensor_scalar(out=var_eps[:], in0=var[:], scalar1=EPS, scalar2=1.0, op0=ALU.add, op1=ALU.mult)
+            rstd = stats.tile([P, 1], F32, name="rstd")
+            nc.gpsimd.tensor_tensor(out=rstd[:], in0=var_eps[:], in1=neg_half[:], op=ALU.pow)
+
+            tanh_c = work.tile([P, HIDDEN], F32, name="tanh_c", bufs=BATCH_TILES)
+            for half in range(HALVES):
+                cols = slice(half * CHUNK, (half + 1) * CHUNK)
+                nc.vector.scalar_tensor_tensor(
+                    out=c_t[:, cols], in0=c_t[:, cols], scalar=rstd[:],
+                    in1=spread[:, LN_B0 + half * CHUNK : LN_B0 + (half + 1) * CHUNK],
+                    op0=ALU.mult, op1=ALU.add,
+                )
+                nc.sync.dma_start(out=out_1[batch_rows, cols], in_=c_t[:, cols])
+                nc.scalar.activation(out=tanh_c[:, cols], in_=c_t[:, cols], func=ACT.Tanh)
+            return tanh_c
+
+        tanh_c = {}
+        for phase, tiles in enumerate(PHASES):
+            u = {}
+            u_sum = {}
+            for m in tiles:
+                u[m] = work.tile([P, HIDDEN], F32, name="u", bufs=3)
+                u_sum[m] = stats.tile([P, HALVES], F32, name="u_sum")
+
+            for half in range(HALVES):
+                cols = slice(half * CHUNK, (half + 1) * CHUNK)
+                value = {}
+                for gate in CELL_GATES:
+                    for m in tiles:
+                        value[(m, gate)] = gate_chunk(m, gate, half)
+                for m in tiles:
+                    ig = work.tile([P, CHUNK], F32, name="ig", bufs=3)
+                    nc.gpsimd.tensor_tensor(out=ig[:], in0=value[(m, GATE_I)][:], in1=value[(m, GATE_G)][:], op=ALU.mult)
+                    nc.gpsimd.tensor_tensor(out=u[m][:, cols], in0=value[(m, GATE_F)][:], in1=c_sb[:, m, cols], op=ALU.mult)
+                    nc.vector.scalar_tensor_tensor(
+                        out=u[m][:, cols], in0=u[m][:, cols], scalar=1.0, in1=ig[:],
+                        op0=ALU.mult, op1=ALU.add, accum_out=u_sum[m][:, half : half + 1],
+                    )
+
+            if phase == 0:
+                for later in PHASES[1:]:
+                    for m in later:
+                        quantise_batch_tile(m)
+
+            for m in tiles:
+                tanh_c[m] = layer_norm(m, u[m], u_sum[m])
+
+        for m in range(BATCH_TILES):
+            for half in range(HALVES):
+                cols = slice(half * CHUNK, (half + 1) * CHUNK)
+                o = gate_chunk(m, GATE_O, half)
+                nc.vector.tensor_tensor(out=tanh_c[m][:, cols], in0=tanh_c[m][:, cols], in1=o[:], op=ALU.mult)
+                nc.sync.dma_start(out=out_0[m * P : (m + 1) * P, cols], in_=tanh_c[m][:, cols])

@@ -227,8 +227,8 @@ def tile_lstmcelllayernorm_kernel(
                         value[(m, gate)] = gate_chunk(m, gate, half)
                 for m in tiles:
                     ig = work.tile([P, CHUNK], F32, name="ig", bufs=3)
-                    nc.gpsimd.tensor_tensor(out=ig[:], in0=value[(m, GATE_I)][:], in1=value[(m, GATE_G)][:], op=ALU.mult)
-                    nc.gpsimd.tensor_tensor(out=u[m][:, cols], in0=value[(m, GATE_F)][:], in1=c_sb[:, m, cols], op=ALU.mult)
+                    nc.vector.tensor_tensor(out=ig[:], in0=value[(m, GATE_I)][:], in1=value[(m, GATE_G)][:], op=ALU.mult)
+                    nc.vector.tensor_tensor(out=u[m][:, cols], in0=value[(m, GATE_F)][:], in1=c_sb[:, m, cols], op=ALU.mult)
                     nc.vector.scalar_tensor_tensor(
                         out=u[m][:, cols], in0=u[m][:, cols], scalar=1.0, in1=ig[:],
                         op0=ALU.mult, op1=ALU.add, accum_out=u_sum[m][:, half : half + 1],

@@ -21,13 +21,14 @@ GROUPS = HIDDEN // (P * PACK)
 K_GROUPS = 2 * GROUPS
 CHUNK = 512
 HALVES = HIDDEN // CHUNK
+BLOCKS = CHUNK // P
+SIDE = 2
+SIDE_ROWS = SIDE * P
+SIDES = BATCH_TILES // SIDE
 EPS = 1e-5
 
 GATE_I, GATE_F, GATE_O, GATE_G = 0, 1, 2, 3
-
 CELL_GATES = (GATE_I, GATE_G, GATE_F)
-
-PHASES = ((0, 1), (2,), (3,))
 
 FLOPS = 2 * BATCH * (2 * HIDDEN) * (4 * HIDDEN)
 
@@ -38,12 +39,12 @@ def tile_lstmcelllayernorm_kernel(
     nc = tc.nc
     with ExitStack() as stack:
         keep = stack.enter_context(tc.tile_pool(name="keep", bufs=1))
-        stage = stack.enter_context(tc.tile_pool(name="stage", bufs=2))
+        stage = stack.enter_context(tc.tile_pool(name="stage", bufs=4))
         gates = stack.enter_context(tc.tile_pool(name="gates", bufs=4))
         work = stack.enter_context(tc.tile_pool(name="work", bufs=2))
         stats = stack.enter_context(tc.tile_pool(name="stats", bufs=4))
-        psum_acc = stack.enter_context(tc.psum_pool(name="psum_acc", bufs=6))
-        psum_flip = stack.enter_context(tc.psum_pool(name="psum_flip", bufs=2))
+        psum_acc = stack.enter_context(tc.psum_pool(name="psum_acc", bufs=3))
+        psum_flip = stack.enter_context(tc.psum_pool(name="psum_flip", bufs=5))
 
         warm = keep.tile([P, 1], F32, name="warm")
         nc.vector.memset(warm[:], 0.0)
@@ -51,8 +52,6 @@ def tile_lstmcelllayernorm_kernel(
 
         ident = keep.tile([P, P], F32, name="ident")
         make_identity(nc, ident[:])
-        ones = keep.tile([P, P], BF16, name="ones")
-        nc.vector.memset(ones[:], 1.0)
         neg_half = keep.tile([P, 1], F32, name="neg_half")
         nc.gpsimd.memset(neg_half[:], -0.5)
 
@@ -86,43 +85,44 @@ def tile_lstmcelllayernorm_kernel(
                         in_=scales[:, 4 * quadrant : 4 * quadrant + 4, :].bitcast(I32),
                     )
 
-        VECTOR_COLS = 4 * HIDDEN + 2 * HIDDEN
-        LN_W0 = 4 * HIDDEN
-        LN_B0 = 5 * HIDDEN
-        rows = keep.tile([P, VECTOR_COLS], BF16, name="rows")
-        nc.vector.memset(rows[:], 0.0)
-        nc.scalar.dma_start(out=rows[0:1, 0 : 4 * HIDDEN], in_=b_ih.unsqueeze(0))
-        nc.scalar.dma_start(out=rows[1:2, 0 : 4 * HIDDEN], in_=b_hh.unsqueeze(0))
-        nc.scalar.dma_start(out=rows[0:1, LN_W0 : LN_W0 + HIDDEN], in_=ln_w.unsqueeze(0))
-        nc.scalar.dma_start(out=rows[0:1, LN_B0 : LN_B0 + HIDDEN], in_=ln_b.unsqueeze(0))
+        N_BLOCKS = 4 * HIDDEN // P
+        bias_rows = keep.tile([P, P], BF16, name="bias_rows")
+        nc.vector.memset(bias_rows[:], 0.0)
+        nc.scalar.dma_start(out=bias_rows[0:N_BLOCKS, :], in_=b_ih.rearrange("(r n) -> r n", n=P))
+        nc.scalar.dma_start(out=bias_rows[N_BLOCKS : 2 * N_BLOCKS, :], in_=b_hh.rearrange("(r n) -> r n", n=P))
+        norm_rows = keep.tile([P, 2 * HIDDEN], BF16, name="norm_rows")
+        nc.vector.memset(norm_rows[:], 0.0)
+        nc.scalar.dma_start(out=norm_rows[0:1, 0:HIDDEN], in_=ln_w.unsqueeze(0))
+        nc.scalar.dma_start(out=norm_rows[0:1, HIDDEN : 2 * HIDDEN], in_=ln_b.unsqueeze(0))
+        ones = keep.tile([P, P], BF16, name="ones")
+        nc.vector.memset(ones[:], 1.0)
 
-        for m in PHASES[0]:
+        for m in range(SIDE):
             load_batch_tile(x_sb, x, m)
             load_batch_tile(h_sb, h, m)
         load_weight_scales()
         for gate in CELL_GATES:
             load_weight_chunk(gate, 0)
-        for m in range(BATCH_TILES):
+        for m in range(SIDE):
             load_batch_tile(c_sb, c, m)
-        for tiles in PHASES[1:]:
-            for m in tiles:
-                load_batch_tile(x_sb, x, m)
-                load_batch_tile(h_sb, h, m)
+        for m in range(SIDE, BATCH_TILES):
+            load_batch_tile(x_sb, x, m)
+            load_batch_tile(h_sb, h, m)
         for gate in CELL_GATES:
             load_weight_chunk(gate, 1)
+        for m in range(SIDE, BATCH_TILES):
+            load_batch_tile(c_sb, c, m)
         for half in range(HALVES):
             load_weight_chunk(GATE_O, half)
 
-        xh_codes = keep.tile([P, BATCH_TILES, K_GROUPS * P], U32, name="xh_codes", align_bytes=64)
-        xh_scales = keep.tile([P, BATCH_TILES, K_GROUPS * P], U8, name="xh_scales", align_bytes=64)
+        xh_codes = keep.tile([P, K_GROUPS, BATCH], U32, name="xh_codes", align_bytes=64)
+        xh_scales = keep.tile([P, K_GROUPS, BATCH], U8, name="xh_scales", align_bytes=64)
 
         def quantise_batch_tile(m):
-            grouped = stage.tile([P, K_GROUPS, P, PACK], BF16, name="grouped", align_bytes=64)
-            grouped_words = grouped[:].bitcast(F32)
+            per_group = HIDDEN // 2 // GROUPS
             for w, src in enumerate((x_sb, h_sb)):
                 words = src[:, m, :].bitcast(F32)
-                per_group = HIDDEN // 2 // GROUPS
-                flipped = psum_flip.tile([P, GROUPS, 2, P], F32, name="flipped")
+                flipped = psum_flip.tile([P, GROUPS, 2, P], F32, name="flipped", tag="flip")
                 for g in range(GROUPS):
                     for u in range(2):
                         nc.tensor.transpose(
@@ -130,53 +130,94 @@ def tile_lstmcelllayernorm_kernel(
                             words[:, per_group * g + u : per_group * (g + 1) : 2],
                             ident[:],
                         )
-                dst = grouped_words[:, GROUPS * w : GROUPS * (w + 1), :, :]
-                pairs = flipped[:].rearrange("p g u r -> p g r u")
-                nc.scalar.copy(out=dst, in_=pairs)
-            nc.vector.quantize_mx(
-                out=xh_codes[:, m, :].bitcast(FP8X4),
-                scales=xh_scales[:, m, :],
-                in_=grouped[:].rearrange("p g r t -> p (g r t)"),
-            )
+                grouped = stage.tile([P, GROUPS, P, PACK], BF16, name="grouped", align_bytes=64)
+                nc.scalar.copy(out=grouped[:].bitcast(F32), in_=flipped[:].rearrange("p g u r -> p g r u"))
+                for g in range(GROUPS):
+                    kg = GROUPS * w + g
+                    nc.vector.quantize_mx(
+                        out=xh_codes[:, kg, m * P : (m + 1) * P].bitcast(FP8X4),
+                        scales=xh_scales[:, kg, m * P : (m + 1) * P],
+                        in_=grouped[:, g, :, :].rearrange("p r t -> p (r t)"),
+                    )
 
-        for m in PHASES[0]:
+        for m in range(SIDE):
             quantise_batch_tile(m)
 
-        spread = keep.tile([P, VECTOR_COLS], F32, name="spread")
-        spread_order = [gate * HIDDEN + half * CHUNK for half in range(HALVES) for gate in CELL_GATES]
-        spread_order += [first + half * CHUNK for first in (LN_W0, LN_B0, GATE_O * HIDDEN) for half in range(HALVES)]
-        for position, col0 in enumerate(spread_order):
-            summed = psum_acc.tile([P, CHUNK], F32, name="acc")
-            nc.tensor.matmul(out=summed[:], lhsT=ones[:], rhs=rows[:, col0 : col0 + CHUNK], start=True, stop=True)
-            if position % 2 == 0:
-                nc.vector.tensor_copy(out=spread[:, col0 : col0 + CHUNK], in_=summed[:])
-            else:
-                nc.scalar.copy(out=spread[:, col0 : col0 + CHUNK], in_=summed[:])
+        pick = keep.tile([P, N_BLOCKS], BF16, name="pick")
+        nc.vector.tensor_tensor(out=pick[:], in0=ident[:, 0:N_BLOCKS], in1=ident[:, N_BLOCKS : 2 * N_BLOCKS], op=ALU.add)
+        bias_sum = psum_acc.tile([P, N_BLOCKS], F32, name="bias_sum", tag="acc")
+        nc.tensor.matmul(out=bias_sum[:], lhsT=bias_rows[:], rhs=pick[:], start=True, stop=True)
+        bias = keep.tile([P, N_BLOCKS], F32, name="bias")
+        nc.vector.tensor_copy(out=bias[:], in_=bias_sum[:])
+        norm = keep.tile([P, 2 * HIDDEN], F32, name="norm")
+        for col0 in range(0, 2 * HIDDEN, CHUNK):
+            copies = psum_acc.tile([P, CHUNK], F32, name="copies", tag="acc")
+            nc.tensor.matmul(out=copies[:], lhsT=ones[:], rhs=norm_rows[:, col0 : col0 + CHUNK], start=True, stop=True)
+            nc.vector.tensor_copy(out=norm[:, col0 : col0 + CHUNK], in_=copies[:])
+        gain = norm[:, 0:HIDDEN]
+        shift = norm[:, HIDDEN : 2 * HIDDEN]
 
-        def gate_chunk(m, gate, half):
-            col0 = gate * HIDDEN + half * CHUNK
-            acc = psum_acc.tile([P, CHUNK], F32, name="acc")
-            for kg in range(K_GROUPS):
-                nc.tensor.matmul_mx(
-                    out=acc[:],
-                    lhsT=xh_codes[:, m, kg * P : (kg + 1) * P].bitcast(FP8X4),
-                    lhsT_scale=xh_scales[:, m, kg * P : (kg + 1) * P],
-                    rhs=w_words[:, kg, col0 : col0 + CHUNK].bitcast(FP8X4),
-                    rhs_scale=w_scales[4 * kg : P, col0 : col0 + CHUNK],
-                    start=(kg == 0),
-                    stop=(kg == K_GROUPS - 1),
+        def gate_half(gate, half, side):
+            rows = slice(side * SIDE_ROWS, (side + 1) * SIDE_ROWS)
+            func = ACT.Tanh if gate == GATE_G else ACT.Sigmoid
+            pieces = []
+            for piece in range(BLOCKS // 2):
+                acc = psum_acc.tile([P, 2, SIDE_ROWS], F32, name="acc", tag="acc")
+                first_block = gate * (HIDDEN // P) + half * BLOCKS + 2 * piece
+                for s in range(2):
+                    cols = slice((first_block + s) * P, (first_block + s + 1) * P)
+                    for kg in range(K_GROUPS):
+                        nc.tensor.matmul_mx(
+                            out=acc[:, s, :],
+                            lhsT=w_words[:, kg, cols].bitcast(FP8X4),
+                            lhsT_scale=w_scales[4 * kg : P, cols],
+                            rhs=xh_codes[:, kg, rows].bitcast(FP8X4),
+                            rhs_scale=xh_scales[:, kg, rows],
+                            start=(kg == 0),
+                            stop=(kg == K_GROUPS - 1),
+                        )
+                value = gates.tile([P, 2, SIDE_ROWS], F32, name="gate%d" % gate)
+                for s in range(2):
+                    block = first_block + s
+                    nc.scalar.activation(out=value[:, s, :], in_=acc[:, s, :], func=func, bias=bias[:, block : block + 1])
+                pieces.append(value)
+            return pieces
+
+        def to_rows(pieces):
+            banks = []
+            for t in range(SIDE):
+                bank = psum_flip.tile([P, BLOCKS, P], F32, name="bank", tag="flip")
+                for q in range(BLOCKS):
+                    nc.tensor.transpose(bank[:, q, :], pieces[q // 2][:, q % 2, t * P : (t + 1) * P], ident[:])
+                banks.append(bank[:].rearrange("p q j -> p (q j)"))
+            return banks
+
+        u = {}
+        u_sum = {}
+        c_t = {}
+        rstd = {}
+        tanh_c = {}
+
+        def cell_update(ig_T, f_T, half, side):
+            cols = slice(half * CHUNK, (half + 1) * CHUNK)
+            ig_rows = to_rows(ig_T)
+            f_rows = to_rows(f_T)
+            tiles = range(side * SIDE, (side + 1) * SIDE)
+            for t, m in enumerate(tiles):
+                if half == 0:
+                    u[m] = work.tile([P, HIDDEN], F32, name="u", bufs=BATCH_TILES)
+                    u_sum[m] = stats.tile([P, HALVES], F32, name="u_sum")
+                nc.vector.tensor_tensor(out=u[m][:, cols], in0=f_rows[t], in1=c_sb[:, m, cols], op=ALU.mult)
+            for t, m in enumerate(tiles):
+                nc.vector.scalar_tensor_tensor(
+                    out=u[m][:, cols], in0=ig_rows[t], scalar=1.0, in1=u[m][:, cols],
+                    op0=ALU.mult, op1=ALU.add, accum_out=u_sum[m][:, half : half + 1],
                 )
-            gate_name = "gate%d" % gate
-            value = gates.tile([P, CHUNK], F32, name=gate_name)
-            nc.vector.tensor_tensor(out=value[:], in0=acc[:], in1=spread[:, col0 : col0 + CHUNK], op=ALU.add)
-            nc.scalar.activation(out=value[:], in_=value[:], func=(ACT.Tanh if gate == GATE_G else ACT.Sigmoid))
-            return value
 
-        def layer_norm(m, u, u_sum):
-            batch_rows = slice(m * P, (m + 1) * P)
+        def start_norm(m):
             neg_mean = stats.tile([P, 1], F32, name="neg_mean")
             nc.vector.tensor_scalar(
-                out=neg_mean[:], in0=u_sum[:, 0:1], scalar1=u_sum[:, 1:2], scalar2=-1.0 / HIDDEN,
+                out=neg_mean[:], in0=u_sum[m][:, 0:1], scalar1=u_sum[m][:, 1:2], scalar2=-1.0 / HIDDEN,
                 op0=ALU.add, op1=ALU.mult,
             )
             neg_mean_scaled = stats.tile([P, 1], F32, name="neg_mean_scaled")
@@ -186,65 +227,72 @@ def tile_lstmcelllayernorm_kernel(
             squares = work.tile([P, HIDDEN], BF16, name="squares")
             var = stats.tile([P, 1], F32, name="var")
             nc.scalar.activation(
-                out=squares[:], in_=u[:], func=ACT.Square, bias=neg_mean_scaled[:], scale=HIDDEN**-0.5,
+                out=squares[:], in_=u[m][:], func=ACT.Square, bias=neg_mean_scaled[:], scale=HIDDEN**-0.5,
                 accum_out=var[:],
             )
-            c_t = work.tile([P, HIDDEN], F32, name="c_t")
+            c_t[m] = work.tile([P, HIDDEN], F32, name="c_t", bufs=3)
             nc.vector.scalar_tensor_tensor(
-                out=c_t[:], in0=u[:], scalar=neg_mean[:], in1=spread[:, LN_W0 : LN_W0 + HIDDEN],
-                op0=ALU.add, op1=ALU.mult,
+                out=c_t[m][:], in0=u[m][:], scalar=neg_mean[:], in1=gain, op0=ALU.add, op1=ALU.mult
             )
             var_eps = stats.tile([P, 1], F32, name="var_eps")
             nc.gpsimd.tensor_scalar(out=var_eps[:], in0=var[:], scalar1=EPS, scalar2=1.0, op0=ALU.add, op1=ALU.mult)
-            rstd = stats.tile([P, 1], F32, name="rstd")
-            nc.gpsimd.tensor_tensor(out=rstd[:], in0=var_eps[:], in1=neg_half[:], op=ALU.pow)
+            rstd[m] = stats.tile([P, 1], F32, name="rstd")
+            nc.gpsimd.tensor_tensor(out=rstd[m][:], in0=var_eps[:], in1=neg_half[:], op=ALU.pow)
 
-            tanh_c = work.tile([P, HIDDEN], F32, name="tanh_c", bufs=BATCH_TILES)
+        def finish_norm(m):
+            tanh_c[m] = work.tile([P, HIDDEN], F32, name="tanh_c", bufs=BATCH_TILES)
             for half in range(HALVES):
                 cols = slice(half * CHUNK, (half + 1) * CHUNK)
                 nc.vector.scalar_tensor_tensor(
-                    out=c_t[:, cols], in0=c_t[:, cols], scalar=rstd[:],
-                    in1=spread[:, LN_B0 + half * CHUNK : LN_B0 + (half + 1) * CHUNK],
+                    out=c_t[m][:, cols], in0=c_t[m][:, cols], scalar=rstd[m][:], in1=shift[:, cols],
                     op0=ALU.mult, op1=ALU.add,
                 )
-                nc.sync.dma_start(out=out_1[batch_rows, cols], in_=c_t[:, cols])
-                nc.scalar.activation(out=tanh_c[:, cols], in_=c_t[:, cols], func=ACT.Tanh)
-            return tanh_c
+                nc.sync.dma_start(out=out_1[m * P : (m + 1) * P, cols], in_=c_t[m][:, cols])
+                nc.scalar.activation(out=tanh_c[m][:, cols], in_=c_t[m][:, cols], func=ACT.Tanh)
 
-        tanh_c = {}
-        for phase, tiles in enumerate(PHASES):
-            u = {}
-            u_sum = {}
-            for m in tiles:
-                u[m] = work.tile([P, HIDDEN], F32, name="u", bufs=3)
-                u_sum[m] = stats.tile([P, HALVES], F32, name="u_sum")
-
-            for half in range(HALVES):
-                cols = slice(half * CHUNK, (half + 1) * CHUNK)
-                value = {}
-                for gate in CELL_GATES:
-                    for m in tiles:
-                        value[(m, gate)] = gate_chunk(m, gate, half)
-                for m in tiles:
-                    ig = work.tile([P, CHUNK], F32, name="ig", bufs=3)
-                    nc.vector.tensor_tensor(out=ig[:], in0=value[(m, GATE_I)][:], in1=value[(m, GATE_G)][:], op=ALU.mult)
-                    nc.vector.tensor_tensor(out=u[m][:, cols], in0=value[(m, GATE_F)][:], in1=c_sb[:, m, cols], op=ALU.mult)
-                    nc.vector.scalar_tensor_tensor(
-                        out=u[m][:, cols], in0=u[m][:, cols], scalar=1.0, in1=ig[:],
-                        op0=ALU.mult, op1=ALU.add, accum_out=u_sum[m][:, half : half + 1],
-                    )
-
-            if phase == 0:
-                for later in PHASES[1:]:
-                    for m in later:
-                        quantise_batch_tile(m)
-
-            for m in tiles:
-                tanh_c[m] = layer_norm(m, u[m], u_sum[m])
-
-        for m in range(BATCH_TILES):
-            for half in range(HALVES):
-                cols = slice(half * CHUNK, (half + 1) * CHUNK)
-                o = gate_chunk(m, GATE_O, half)
-                nc.vector.tensor_tensor(out=tanh_c[m][:, cols], in0=tanh_c[m][:, cols], in1=o[:], op=ALU.mult)
+        def output(o_T, half, side):
+            cols = slice(half * CHUNK, (half + 1) * CHUNK)
+            o_rows = to_rows(o_T)
+            for t, m in enumerate(range(side * SIDE, (side + 1) * SIDE)):
+                nc.vector.tensor_tensor(out=tanh_c[m][:, cols], in0=o_rows[t], in1=tanh_c[m][:, cols], op=ALU.mult)
                 nc.sync.dma_start(out=out_0[m * P : (m + 1) * P, cols], in_=tanh_c[m][:, cols])
+
+        steps = [(side, half) for side in range(SIDES) for half in range(HALVES)]
+        waiting = None
+        for side, half in steps:
+            i_T = gate_half(GATE_I, half, side)
+            if waiting is not None:
+                cell_update(*waiting)
+            if side > 0 and half == 0:
+                for m in range((side - 1) * SIDE, side * SIDE):
+                    start_norm(m)
+            if side > 0 and half == 1:
+                for m in range((side - 1) * SIDE, side * SIDE):
+                    finish_norm(m)
+            g_T = gate_half(GATE_G, half, side)
+            if side == 0 and half == 1:
+                for m in range(SIDE, BATCH_TILES):
+                    quantise_batch_tile(m)
+            f_T = gate_half(GATE_F, half, side)
+            ig_T = []
+            for piece in range(BLOCKS // 2):
+                product = gates.tile([P, 2, SIDE_ROWS], F32, name="product")
+                nc.vector.tensor_tensor(out=product[:], in0=i_T[piece][:], in1=g_T[piece][:], op=ALU.mult)
+                ig_T.append(product)
+            waiting = (ig_T, f_T, half, side)
+
+        last_tiles = range((SIDES - 1) * SIDE, SIDES * SIDE)
+        waiting_o = None
+        for position, (side, half) in enumerate(steps):
+            o_T = gate_half(GATE_O, half, side)
+            if position == 0:
+                cell_update(*waiting)
+                for m in last_tiles:
+                    start_norm(m)
+            if waiting_o is not None:
+                output(*waiting_o)
+            if position == 1:
+                for m in last_tiles:
+                    finish_norm(m)
+            waiting_o = (o_T, half, side)
+        output(*waiting_o)

@@ -38,6 +38,7 @@ def tile_lstmcelllayernorm_kernel(
 ):
     nc = tc.nc
     with ExitStack() as stack:
+        stack.enter_context(tc.manual_schedule())
         keep = stack.enter_context(tc.tile_pool(name="keep", bufs=1))
         stage = stack.enter_context(tc.tile_pool(name="stage", bufs=4))
         gates = stack.enter_context(tc.tile_pool(name="gates", bufs=4))

@@ -38,14 +38,13 @@ def tile_lstmcelllayernorm_kernel(
 ):
     nc = tc.nc
     with ExitStack() as stack:
-        stack.enter_context(tc.manual_schedule())
         keep = stack.enter_context(tc.tile_pool(name="keep", bufs=1))
         stage = stack.enter_context(tc.tile_pool(name="stage", bufs=4))
         gates = stack.enter_context(tc.tile_pool(name="gates", bufs=4))
         work = stack.enter_context(tc.tile_pool(name="work", bufs=2))
         stats = stack.enter_context(tc.tile_pool(name="stats", bufs=4))
-        psum_acc = stack.enter_context(tc.psum_pool(name="psum_acc", bufs=3))
-        psum_flip = stack.enter_context(tc.psum_pool(name="psum_flip", bufs=5))
+        psum_acc = stack.enter_context(tc.psum_pool(name="psum_acc", bufs=4))
+        psum_flip = stack.enter_context(tc.psum_pool(name="psum_flip", bufs=4))
 
         warm = keep.tile([P, 1], F32, name="warm")
         nc.vector.memset(warm[:], 0.0)
@@ -60,19 +59,22 @@ def tile_lstmcelllayernorm_kernel(
         h_sb = keep.tile([P, BATCH_TILES, HIDDEN], BF16, name="h_sb")
         c_sb = keep.tile([P, BATCH_TILES, HIDDEN], BF16, name="c_sb")
 
-        def load_batch_tile(dst, src, m):
-            nc.sync.dma_start(out=dst[:, m, :], in_=src[m * P : (m + 1) * P, :])
+        def load_side(dst, src, side):
+            tiles = slice(side * SIDE, (side + 1) * SIDE)
+            nc.sync.dma_start(out=dst[:, tiles, :], in_=src.rearrange("(m p) k -> p m k", p=P)[:, tiles, :])
 
         w_words = keep.tile([P, K_GROUPS, 4 * HIDDEN], U32, name="w_words", align_bytes=64)
 
-        def load_weight_chunk(gate, half):
-            col0 = gate * HIDDEN + half * CHUNK
+        def load_weight_columns(col0, width):
             for w, words in enumerate((W_ih_words, W_hh_words)):
                 by_partition = words.rearrange("g p n t -> p g (n t)")
                 nc.sync.dma_start(
-                    out=w_words[:, GROUPS * w : GROUPS * (w + 1), col0 : col0 + CHUNK].bitcast(I32),
-                    in_=by_partition[:, :, PACK * col0 : PACK * (col0 + CHUNK)].bitcast(I32),
+                    out=w_words[:, GROUPS * w : GROUPS * (w + 1), col0 : col0 + width].bitcast(I32),
+                    in_=by_partition[:, :, PACK * col0 : PACK * (col0 + width)].bitcast(I32),
                 )
+
+        def load_weight_chunk(gate, half):
+            load_weight_columns(gate * HIDDEN + half * CHUNK, CHUNK)
 
         w_scales = keep.tile([P, 4 * HIDDEN], U8, name="w_scales", align_bytes=64)
         nc.vector.memset(w_scales[:].bitcast(I32), 0)
@@ -89,32 +91,33 @@ def tile_lstmcelllayernorm_kernel(
         N_BLOCKS = 4 * HIDDEN // P
         bias_rows = keep.tile([P, P], BF16, name="bias_rows")
         nc.vector.memset(bias_rows[:], 0.0)
-        nc.scalar.dma_start(out=bias_rows[0:N_BLOCKS, :], in_=b_ih.rearrange("(r n) -> r n", n=P))
-        nc.scalar.dma_start(out=bias_rows[N_BLOCKS : 2 * N_BLOCKS, :], in_=b_hh.rearrange("(r n) -> r n", n=P))
-        norm_rows = keep.tile([P, 2 * HIDDEN], BF16, name="norm_rows")
-        nc.vector.memset(norm_rows[:], 0.0)
-        nc.scalar.dma_start(out=norm_rows[0:1, 0:HIDDEN], in_=ln_w.unsqueeze(0))
-        nc.scalar.dma_start(out=norm_rows[0:1, HIDDEN : 2 * HIDDEN], in_=ln_b.unsqueeze(0))
-        ones = keep.tile([P, P], BF16, name="ones")
-        nc.vector.memset(ones[:], 1.0)
 
-        for m in range(SIDE):
-            load_batch_tile(x_sb, x, m)
-            load_batch_tile(h_sb, h, m)
-        load_weight_scales()
-        for gate in CELL_GATES:
-            load_weight_chunk(gate, 0)
-        for m in range(SIDE):
-            load_batch_tile(c_sb, c, m)
-        for m in range(SIDE, BATCH_TILES):
-            load_batch_tile(x_sb, x, m)
-            load_batch_tile(h_sb, h, m)
-        for gate in CELL_GATES:
-            load_weight_chunk(gate, 1)
-        for m in range(SIDE, BATCH_TILES):
-            load_batch_tile(c_sb, c, m)
-        for half in range(HALVES):
-            load_weight_chunk(GATE_O, half)
+        def load_biases():
+            nc.sync.dma_start(out=bias_rows[0:N_BLOCKS, :], in_=b_ih.rearrange("(r n) -> r n", n=P))
+            nc.sync.dma_start(out=bias_rows[N_BLOCKS : 2 * N_BLOCKS, :], in_=b_hh.rearrange("(r n) -> r n", n=P))
+
+        gain = keep.tile([P, HIDDEN], BF16, name="gain")
+        shift = keep.tile([P, HIDDEN], BF16, name="shift")
+
+        with tc.manual_schedule():
+            load_side(x_sb, x, 0)
+            load_side(h_sb, h, 0)
+            load_weight_scales()
+            load_weight_columns(GATE_I * HIDDEN, CHUNK // 2)
+            load_biases()
+            load_weight_columns(GATE_I * HIDDEN + CHUNK // 2, CHUNK // 2)
+            load_side(x_sb, x, 1)
+            load_side(h_sb, h, 1)
+            load_weight_chunk(GATE_G, 0)
+            load_weight_chunk(GATE_F, 0)
+            for side in range(SIDES):
+                load_side(c_sb, c, side)
+            for gate in CELL_GATES:
+                load_weight_chunk(gate, 1)
+            for half in range(HALVES):
+                load_weight_chunk(GATE_O, half)
+            nc.sync.dma_start(out=gain[:], in_=ln_w.partition_broadcast(P))
+            nc.sync.dma_start(out=shift[:], in_=ln_b.partition_broadcast(P))
 
         xh_codes = keep.tile([P, K_GROUPS, BATCH], U32, name="xh_codes", align_bytes=64)
         xh_scales = keep.tile([P, K_GROUPS, BATCH], U8, name="xh_scales", align_bytes=64)
@@ -150,13 +153,18 @@ def tile_lstmcelllayernorm_kernel(
         nc.tensor.matmul(out=bias_sum[:], lhsT=bias_rows[:], rhs=pick[:], start=True, stop=True)
         bias = keep.tile([P, N_BLOCKS], F32, name="bias")
         nc.vector.tensor_copy(out=bias[:], in_=bias_sum[:])
-        norm = keep.tile([P, 2 * HIDDEN], F32, name="norm")
-        for col0 in range(0, 2 * HIDDEN, CHUNK):
-            copies = psum_acc.tile([P, CHUNK], F32, name="copies", tag="acc")
-            nc.tensor.matmul(out=copies[:], lhsT=ones[:], rhs=norm_rows[:, col0 : col0 + CHUNK], start=True, stop=True)
-            nc.vector.tensor_copy(out=norm[:, col0 : col0 + CHUNK], in_=copies[:])
-        gain = norm[:, 0:HIDDEN]
-        shift = norm[:, HIDDEN : 2 * HIDDEN]
+        f_bias = keep.tile([P, HIDDEN], F32, name="f_bias")
+        for half in range(HALVES):
+            summed = psum_acc.tile([P, BLOCKS, P], F32, name="summed", tag="acc")
+            for q in range(BLOCKS):
+                block = GATE_F * (HIDDEN // P) + half * BLOCKS + q
+                nc.tensor.matmul(
+                    out=summed[:, q, :], lhsT=pick[:, block : block + 1].to_broadcast([P, P]), rhs=bias_rows[:],
+                    start=True, stop=True,
+                )
+            nc.vector.tensor_copy(
+                out=f_bias[:, half * CHUNK : (half + 1) * CHUNK], in_=summed[:].rearrange("p q n -> p (q n)")
+            )
 
         def gate_half(gate, half, side):
             rows = slice(side * SIDE_ROWS, (side + 1) * SIDE_ROWS)
@@ -177,7 +185,7 @@ def tile_lstmcelllayernorm_kernel(
                             start=(kg == 0),
                             stop=(kg == K_GROUPS - 1),
                         )
-                value = gates.tile([P, 2, SIDE_ROWS], F32, name="gate%d" % gate)
+                value = gates.tile([P, 2, SIDE_ROWS], F32, name="gate%d" % gate, bufs=6)
                 for s in range(2):
                     block = first_block + s
                     nc.scalar.activation(out=value[:, s, :], in_=acc[:, s, :], func=func, bias=bias[:, block : block + 1])
@@ -193,27 +201,50 @@ def tile_lstmcelllayernorm_kernel(
                 banks.append(bank[:].rearrange("p q j -> p (q j)"))
             return banks
 
+        ig_T = {}
+        o_T = {}
         u = {}
         u_sum = {}
         c_t = {}
         rstd = {}
         tanh_c = {}
 
-        def cell_update(ig_T, f_T, half, side):
+        def forget_times_c(half, side):
             cols = slice(half * CHUNK, (half + 1) * CHUNK)
-            ig_rows = to_rows(ig_T)
-            f_rows = to_rows(f_T)
-            tiles = range(side * SIDE, (side + 1) * SIDE)
-            for t, m in enumerate(tiles):
+            w_cols = slice(GATE_F * HIDDEN + half * CHUNK, GATE_F * HIDDEN + (half + 1) * CHUNK)
+            for m in range(side * SIDE, (side + 1) * SIDE):
+                rows = slice(m * P, (m + 1) * P)
+                acc = psum_acc.tile([P, CHUNK], F32, name="acc_rows", tag="acc")
+                for kg in range(K_GROUPS):
+                    nc.tensor.matmul_mx(
+                        out=acc[:],
+                        lhsT=xh_codes[:, kg, rows].bitcast(FP8X4),
+                        lhsT_scale=xh_scales[:, kg, rows],
+                        rhs=w_words[:, kg, w_cols].bitcast(FP8X4),
+                        rhs_scale=w_scales[4 * kg : P, w_cols],
+                        start=(kg == 0),
+                        stop=(kg == K_GROUPS - 1),
+                    )
+                f = gates.tile([P, CHUNK], F32, name="f")
+                nc.vector.tensor_tensor(out=f[:], in0=acc[:], in1=f_bias[:, cols], op=ALU.add)
+                nc.scalar.activation(out=f[:], in_=f[:], func=ACT.Sigmoid)
                 if half == 0:
                     u[m] = work.tile([P, HIDDEN], F32, name="u", bufs=BATCH_TILES)
                     u_sum[m] = stats.tile([P, HALVES], F32, name="u_sum")
-                nc.vector.tensor_tensor(out=u[m][:, cols], in0=f_rows[t], in1=c_sb[:, m, cols], op=ALU.mult)
+                nc.vector.tensor_tensor(out=u[m][:, cols], in0=f[:], in1=c_sb[:, m, cols], op=ALU.mult)
+
+        def add_products(half, side):
+            cols = slice(half * CHUNK, (half + 1) * CHUNK)
+            ig_rows = to_rows(ig_T[(half, side)])
+            tiles = range(side * SIDE, (side + 1) * SIDE)
             for t, m in enumerate(tiles):
                 nc.vector.scalar_tensor_tensor(
                     out=u[m][:, cols], in0=ig_rows[t], scalar=1.0, in1=u[m][:, cols],
                     op0=ALU.mult, op1=ALU.add, accum_out=u_sum[m][:, half : half + 1],
                 )
+            if half == HALVES - 1:
+                for m in tiles:
+                    start_norm(m)
 
         def start_norm(m):
             neg_mean = stats.tile([P, 1], F32, name="neg_mean")
@@ -233,7 +264,7 @@ def tile_lstmcelllayernorm_kernel(
             )
             c_t[m] = work.tile([P, HIDDEN], F32, name="c_t", bufs=3)
             nc.vector.scalar_tensor_tensor(
-                out=c_t[m][:], in0=u[m][:], scalar=neg_mean[:], in1=gain, op0=ALU.add, op1=ALU.mult
+                out=c_t[m][:], in0=u[m][:], scalar=neg_mean[:], in1=gain[:], op0=ALU.add, op1=ALU.mult
             )
             var_eps = stats.tile([P, 1], F32, name="var_eps")
             nc.gpsimd.tensor_scalar(out=var_eps[:], in0=var[:], scalar1=EPS, scalar2=1.0, op0=ALU.add, op1=ALU.mult)
@@ -251,49 +282,48 @@ def tile_lstmcelllayernorm_kernel(
                 nc.sync.dma_start(out=out_1[m * P : (m + 1) * P, cols], in_=c_t[m][:, cols])
                 nc.scalar.activation(out=tanh_c[m][:, cols], in_=c_t[m][:, cols], func=ACT.Tanh)
 
-        def output(o_T, half, side):
+        def output(half, side):
             cols = slice(half * CHUNK, (half + 1) * CHUNK)
-            o_rows = to_rows(o_T)
+            o_rows = to_rows(o_T[(half, side)])
             for t, m in enumerate(range(side * SIDE, (side + 1) * SIDE)):
                 nc.vector.tensor_tensor(out=tanh_c[m][:, cols], in0=o_rows[t], in1=tanh_c[m][:, cols], op=ALU.mult)
                 nc.sync.dma_start(out=out_0[m * P : (m + 1) * P, cols], in_=tanh_c[m][:, cols])
 
-        steps = [(side, half) for side in range(SIDES) for half in range(HALVES)]
-        waiting = None
-        for side, half in steps:
-            i_T = gate_half(GATE_I, half, side)
-            if waiting is not None:
-                cell_update(*waiting)
-            if side > 0 and half == 0:
-                for m in range((side - 1) * SIDE, side * SIDE):
-                    start_norm(m)
-            if side > 0 and half == 1:
-                for m in range((side - 1) * SIDE, side * SIDE):
-                    finish_norm(m)
-            g_T = gate_half(GATE_G, half, side)
-            if side == 0 and half == 1:
-                for m in range(SIDE, BATCH_TILES):
-                    quantise_batch_tile(m)
-            f_T = gate_half(GATE_F, half, side)
-            ig_T = []
-            for piece in range(BLOCKS // 2):
-                product = gates.tile([P, 2, SIDE_ROWS], F32, name="product")
-                nc.vector.tensor_tensor(out=product[:], in0=i_T[piece][:], in1=g_T[piece][:], op=ALU.mult)
-                ig_T.append(product)
-            waiting = (ig_T, f_T, half, side)
+        cell_steps = [(0, (0, 1)), (1, (0,)), (1, (1,))]
+        previous = None
+        for half, sides in cell_steps:
+            i_T = {}
+            for side in sides:
+                i_T[side] = gate_half(GATE_I, half, side)
+                if previous is None and side == 0:
+                    for m in range(SIDE, BATCH_TILES):
+                        quantise_batch_tile(m)
+            if previous is not None:
+                for side in previous[1]:
+                    add_products(previous[0], side)
+            for side in sides:
+                g_T = gate_half(GATE_G, half, side)
+                ig_T[(half, side)] = []
+                for piece in range(BLOCKS // 2):
+                    product = gates.tile([P, 2, SIDE_ROWS], F32, name="product", bufs=6)
+                    nc.vector.tensor_tensor(out=product[:], in0=i_T[side][piece][:], in1=g_T[piece][:], op=ALU.mult)
+                    ig_T[(half, side)].append(product)
+            for side in sides:
+                forget_times_c(half, side)
+            if previous is not None and previous[0] == HALVES - 1:
+                for side in previous[1]:
+                    for m in range(side * SIDE, (side + 1) * SIDE):
+                        finish_norm(m)
+            previous = (half, sides)
 
-        last_tiles = range((SIDES - 1) * SIDE, SIDES * SIDE)
-        waiting_o = None
-        for position, (side, half) in enumerate(steps):
-            o_T = gate_half(GATE_O, half, side)
+        out_steps = [(half, side) for side in range(SIDES) for half in range(HALVES)]
+        for position, (half, side) in enumerate(out_steps):
+            o_T[(half, side)] = gate_half(GATE_O, half, side)
             if position == 0:
-                cell_update(*waiting)
-                for m in last_tiles:
-                    start_norm(m)
-            if waiting_o is not None:
-                output(*waiting_o)
+                add_products(HALVES - 1, SIDES - 1)
+            else:
+                output(*out_steps[position - 1])
             if position == 1:
-                for m in last_tiles:
+                for m in range((SIDES - 1) * SIDE, SIDES * SIDE):
                     finish_norm(m)
-            waiting_o = (o_T, half, side)
-        output(*waiting_o)
+        output(*out_steps[-1])

@@ -77,15 +77,18 @@ def tile_lstmcelllayernorm_kernel(
             load_weight_columns(gate * HIDDEN + half * CHUNK, CHUNK)
 
         w_scales = keep.tile([P, 4 * HIDDEN], U8, name="w_scales", align_bytes=64)
-        nc.vector.memset(w_scales[:].bitcast(I32), 0)
+        first_round = slice(GATE_I * HIDDEN, (GATE_I + 1) * HIDDEN)
+        second_round = slice((GATE_I + 1) * HIDDEN, 4 * HIDDEN)
+        nc.vector.memset(w_scales[:, first_round].bitcast(I32), 0)
+        nc.vector.memset(w_scales[:, second_round].bitcast(I32), 0)
 
-        def load_weight_scales():
+        def load_weight_scales(cols):
             for quadrant in range(4):
                 for w, scales in enumerate((W_ih_scales, W_hh_scales)):
                     first = 32 * quadrant + 4 * GROUPS * w
                     nc.sync.dma_start(
-                        out=w_scales[first : first + 4 * GROUPS, :].bitcast(I32),
-                        in_=scales[:, 4 * quadrant : 4 * quadrant + 4, :].bitcast(I32),
+                        out=w_scales[first : first + 4 * GROUPS, cols].bitcast(I32),
+                        in_=scales[:, 4 * quadrant : 4 * quadrant + 4, cols].bitcast(I32),
                     )
 
         N_BLOCKS = 4 * HIDDEN // P
@@ -102,12 +105,13 @@ def tile_lstmcelllayernorm_kernel(
         with tc.manual_schedule():
             load_side(x_sb, x, 0)
             load_side(h_sb, h, 0)
-            load_weight_scales()
+            load_weight_scales(first_round)
             load_weight_columns(GATE_I * HIDDEN, CHUNK // 2)
             load_biases()
             load_weight_columns(GATE_I * HIDDEN + CHUNK // 2, CHUNK // 2)
             load_side(x_sb, x, 1)
             load_side(h_sb, h, 1)
+            load_weight_scales(second_round)
             load_weight_chunk(GATE_G, 0)
             load_weight_chunk(GATE_F, 0)
             for side in range(SIDES):

@@ -106,11 +106,11 @@ def tile_lstmcelllayernorm_kernel(
             load_side(x_sb, x, 0)
             load_side(h_sb, h, 0)
             load_weight_scales(first_round)
-            load_weight_columns(GATE_I * HIDDEN, CHUNK // 2)
             load_biases()
-            load_weight_columns(GATE_I * HIDDEN + CHUNK // 2, CHUNK // 2)
+            load_weight_columns(GATE_I * HIDDEN, CHUNK // 2)
             load_side(x_sb, x, 1)
             load_side(h_sb, h, 1)
+            load_weight_columns(GATE_I * HIDDEN + CHUNK // 2, CHUNK // 2)
             load_weight_scales(second_round)
             load_weight_chunk(GATE_G, 0)
             load_weight_chunk(GATE_F, 0)
@@ -139,7 +139,10 @@ def tile_lstmcelllayernorm_kernel(
                             ident[:],
                         )
                 grouped = stage.tile([P, GROUPS, P, PACK], BF16, name="grouped", align_bytes=64)
-                nc.scalar.copy(out=grouped[:].bitcast(F32), in_=flipped[:].rearrange("p g u r -> p g r u"))
+                if w == 1 and m < SIDE:
+                    nc.vector.tensor_copy(out=grouped[:].bitcast(F32), in_=flipped[:].rearrange("p g u r -> p g r u"))
+                else:
+                    nc.scalar.copy(out=grouped[:].bitcast(F32), in_=flipped[:].rearrange("p g u r -> p g r u"))
                 for g in range(GROUPS):
                     kg = GROUPS * w + g
                     nc.vector.quantize_mx(
@@ -148,29 +151,30 @@ def tile_lstmcelllayernorm_kernel(
                         in_=grouped[:, g, :, :].rearrange("p r t -> p (r t)"),
                     )
 
-        for m in range(SIDE):
-            quantise_batch_tile(m)
-
         pick = keep.tile([P, N_BLOCKS], BF16, name="pick")
         nc.vector.tensor_tensor(out=pick[:], in0=ident[:, 0:N_BLOCKS], in1=ident[:, N_BLOCKS : 2 * N_BLOCKS], op=ALU.add)
-        bias_sum = psum_acc.tile([P, N_BLOCKS], F32, name="bias_sum", tag="acc")
-        nc.tensor.matmul(out=bias_sum[:], lhsT=bias_rows[:], rhs=pick[:], start=True, stop=True)
         bias = keep.tile([P, N_BLOCKS], F32, name="bias")
-        nc.vector.tensor_copy(out=bias[:], in_=bias_sum[:])
         f_bias = keep.tile([P, HIDDEN], F32, name="f_bias")
-        for half in range(HALVES):
-            summed = psum_acc.tile([P, BLOCKS, P], F32, name="summed", tag="acc")
-            for q in range(BLOCKS):
-                block = GATE_F * (HIDDEN // P) + half * BLOCKS + q
-                nc.tensor.matmul(
-                    out=summed[:, q, :], lhsT=pick[:, block : block + 1].to_broadcast([P, P]), rhs=bias_rows[:],
-                    start=True, stop=True,
-                )
-            nc.vector.tensor_copy(
-                out=f_bias[:, half * CHUNK : (half + 1) * CHUNK], in_=summed[:].rearrange("p q n -> p (q n)")
-            )
 
-        def gate_half(gate, half, side):
+        def lay_out_bias():
+            bias_sum = psum_acc.tile([P, N_BLOCKS], F32, name="bias_sum", tag="acc")
+            nc.tensor.matmul(out=bias_sum[:], lhsT=bias_rows[:], rhs=pick[:], start=True, stop=True)
+            nc.vector.tensor_copy(out=bias[:], in_=bias_sum[:])
+
+        def lay_out_f_bias():
+            for half in range(HALVES):
+                summed = psum_acc.tile([P, BLOCKS, P], F32, name="summed", tag="acc")
+                for q in range(BLOCKS):
+                    block = GATE_F * (HIDDEN // P) + half * BLOCKS + q
+                    nc.tensor.matmul(
+                        out=summed[:, q, :], lhsT=pick[:, block : block + 1].to_broadcast([P, P]), rhs=bias_rows[:],
+                        start=True, stop=True,
+                    )
+                nc.vector.tensor_copy(
+                    out=f_bias[:, half * CHUNK : (half + 1) * CHUNK], in_=summed[:].rearrange("p q n -> p (q n)")
+                )
+
+        def gate_half(gate, half, side, between=None):
             rows = slice(side * SIDE_ROWS, (side + 1) * SIDE_ROWS)
             func = ACT.Tanh if gate == GATE_G else ACT.Sigmoid
             pieces = []
@@ -194,6 +198,8 @@ def tile_lstmcelllayernorm_kernel(
                     block = first_block + s
                     nc.scalar.activation(out=value[:, s, :], in_=acc[:, s, :], func=func, bias=bias[:, block : block + 1])
                 pieces.append(value)
+                if between is not None and piece == 0:
+                    between()
             return pieces
 
         def to_rows(pieces):
@@ -256,22 +262,19 @@ def tile_lstmcelllayernorm_kernel(
                 out=neg_mean[:], in0=u_sum[m][:, 0:1], scalar1=u_sum[m][:, 1:2], scalar2=-1.0 / HIDDEN,
                 op0=ALU.add, op1=ALU.mult,
             )
-            neg_mean_scaled = stats.tile([P, 1], F32, name="neg_mean_scaled")
-            nc.vector.tensor_scalar(
-                out=neg_mean_scaled[:], in0=neg_mean[:], scalar1=HIDDEN**-0.5, scalar2=None, op0=ALU.mult
-            )
             squares = work.tile([P, HIDDEN], BF16, name="squares")
             var = stats.tile([P, 1], F32, name="var")
             nc.scalar.activation(
-                out=squares[:], in_=u[m][:], func=ACT.Square, bias=neg_mean_scaled[:], scale=HIDDEN**-0.5,
-                accum_out=var[:],
+                out=squares[:], in_=u[m][:], func=ACT.Square, bias=neg_mean[:], scale=1.0, accum_out=var[:]
             )
             c_t[m] = work.tile([P, HIDDEN], F32, name="c_t", bufs=3)
             nc.vector.scalar_tensor_tensor(
                 out=c_t[m][:], in0=u[m][:], scalar=neg_mean[:], in1=gain[:], op0=ALU.add, op1=ALU.mult
             )
             var_eps = stats.tile([P, 1], F32, name="var_eps")
-            nc.gpsimd.tensor_scalar(out=var_eps[:], in0=var[:], scalar1=EPS, scalar2=1.0, op0=ALU.add, op1=ALU.mult)
+            nc.gpsimd.tensor_scalar(
+                out=var_eps[:], in0=var[:], scalar1=1.0 / HIDDEN, scalar2=EPS, op0=ALU.mult, op1=ALU.add
+            )
             rstd[m] = stats.tile([P, 1], F32, name="rstd")
             nc.gpsimd.tensor_tensor(out=rstd[m][:], in0=var_eps[:], in1=neg_half[:], op=ALU.pow)
 
@@ -293,15 +296,27 @@ def tile_lstmcelllayernorm_kernel(
                 nc.vector.tensor_tensor(out=tanh_c[m][:, cols], in0=o_rows[t], in1=tanh_c[m][:, cols], op=ALU.mult)
                 nc.sync.dma_start(out=out_0[m * P : (m + 1) * P, cols], in_=tanh_c[m][:, cols])
 
+        def second_side_in():
+            for m in range(SIDE, BATCH_TILES):
+                quantise_batch_tile(m)
+
+        first_i = {}
+        with tc.manual_schedule(engines={mybir.EngineType.PE}):
+            for m in range(SIDE):
+                quantise_batch_tile(m)
+            lay_out_bias()
+            first_i[0] = gate_half(GATE_I, 0, 0, between=second_side_in)
+            lay_out_f_bias()
+            first_i[1] = gate_half(GATE_I, 0, 1)
+
         cell_steps = [(0, (0, 1)), (1, (0,)), (1, (1,))]
         previous = None
         for half, sides in cell_steps:
-            i_T = {}
-            for side in sides:
-                i_T[side] = gate_half(GATE_I, half, side)
-                if previous is None and side == 0:
-                    for m in range(SIDE, BATCH_TILES):
-                        quantise_batch_tile(m)
+            i_T = first_i
+            if previous is not None:
+                i_T = {}
+                for side in sides:
+                    i_T[side] = gate_half(GATE_I, half, side)
             if previous is not None:
                 for side in previous[1]:
                     add_products(previous[0], side)

@@ -114,10 +114,11 @@ def tile_lstmcelllayernorm_kernel(
             load_weight_scales(second_round)
             load_weight_chunk(GATE_G, 0)
             load_weight_chunk(GATE_F, 0)
+            load_weight_chunk(GATE_I, 1)
             for side in range(SIDES):
                 load_side(c_sb, c, side)
-            for gate in CELL_GATES:
-                load_weight_chunk(gate, 1)
+            load_weight_chunk(GATE_G, 1)
+            load_weight_chunk(GATE_F, 1)
             for half in range(HALVES):
                 load_weight_chunk(GATE_O, half)
             nc.sync.dma_start(out=gain[:], in_=ln_w.partition_broadcast(P))

@@ -91,6 +91,15 @@ def tile_lstmcelllayernorm_kernel(
                         in_=scales[:, 4 * quadrant : 4 * quadrant + 4, cols].bitcast(I32),
                     )
 
+        def load_weight_scales_aside(cols):
+            for quadrant in range(4):
+                for w, scales in enumerate((W_ih_scales, W_hh_scales)):
+                    first = 32 * quadrant + 4 * GROUPS * w
+                    nc.gpsimd.dma_start(
+                        out=w_scales[first : first + 4 * GROUPS, cols].bitcast(F32),
+                        in_=scales[:, 4 * quadrant : 4 * quadrant + 4, cols].bitcast(F32),
+                    )
+
         N_BLOCKS = 4 * HIDDEN // P
         bias_rows = keep.tile([P, P], BF16, name="bias_rows")
         nc.vector.memset(bias_rows[:], 0.0)
@@ -111,7 +120,7 @@ def tile_lstmcelllayernorm_kernel(
             load_side(x_sb, x, 1)
             load_side(h_sb, h, 1)
             load_weight_columns(GATE_I * HIDDEN + CHUNK // 2, CHUNK // 2)
-            load_weight_scales(second_round)
+            load_weight_scales_aside(second_round)
             load_weight_chunk(GATE_G, 0)
             load_weight_chunk(GATE_F, 0)
             load_weight_chunk(GATE_I, 1)

@@ -63,7 +63,7 @@ def tile_lstmcelllayernorm_kernel(
             tiles = slice(side * SIDE, (side + 1) * SIDE)
             nc.sync.dma_start(out=dst[:, tiles, :], in_=src.rearrange("(m p) k -> p m k", p=P)[:, tiles, :])
 
-        w_words = keep.tile([P, K_GROUPS, 4 * HIDDEN], U32, name="w_words", align_bytes=64)
+        w_words = keep.tile([P, K_GROUPS, 4 * HIDDEN], U32, name="w_words", align_bytes=256)
 
         def load_weight_columns(col0, width):
             for w, words in enumerate((W_ih_words, W_hh_words)):
@@ -76,7 +76,7 @@ def tile_lstmcelllayernorm_kernel(
         def load_weight_chunk(gate, half):
             load_weight_columns(gate * HIDDEN + half * CHUNK, CHUNK)
 
-        w_scales = keep.tile([P, 4 * HIDDEN], U8, name="w_scales", align_bytes=64)
+        w_scales = keep.tile([P, 4 * HIDDEN], U8, name="w_scales", align_bytes=256)
         first_round = slice(GATE_I * HIDDEN, (GATE_I + 1) * HIDDEN)
         second_round = slice((GATE_I + 1) * HIDDEN, 4 * HIDDEN)
         nc.vector.memset(w_scales[:, first_round].bitcast(I32), 0)
@@ -133,8 +133,8 @@ def tile_lstmcelllayernorm_kernel(
             nc.sync.dma_start(out=gain[:], in_=ln_w.partition_broadcast(P))
             nc.sync.dma_start(out=shift[:], in_=ln_b.partition_broadcast(P))
 
-        xh_codes = keep.tile([P, K_GROUPS, BATCH], U32, name="xh_codes", align_bytes=64)
-        xh_scales = keep.tile([P, K_GROUPS, BATCH], U8, name="xh_scales", align_bytes=64)
+        xh_codes = keep.tile([P, K_GROUPS, BATCH], U32, name="xh_codes", align_bytes=256)
+        xh_scales = keep.tile([P, K_GROUPS, BATCH], U8, name="xh_scales", align_bytes=256)
 
         def quantise_batch_tile(m):
             per_group = HIDDEN // 2 // GROUPS
@@ -148,7 +148,7 @@ def tile_lstmcelllayernorm_kernel(
                             words[:, per_group * g + u : per_group * (g + 1) : 2],
                             ident[:],
                         )
-                grouped = stage.tile([P, GROUPS, P, PACK], BF16, name="grouped", align_bytes=64)
+                grouped = stage.tile([P, GROUPS, P, PACK], BF16, name="grouped", align_bytes=256)
                 if w == 1 and m < SIDE:
                     nc.vector.tensor_copy(out=grouped[:].bitcast(F32), in_=flipped[:].rearrange("p g u r -> p g r u"))
                 else:

@@ -59,6 +59,9 @@ def tile_lstmcelllayernorm_kernel(
         h_sb = keep.tile([P, BATCH_TILES, HIDDEN], BF16, name="h_sb")
         c_sb = keep.tile([P, BATCH_TILES, HIDDEN], BF16, name="c_sb")
 
+        def load_tile(dst, src, m):
+            nc.sync.dma_start(out=dst[:, m, :], in_=src[m * P : (m + 1) * P, :])
+
         def load_side(dst, src, side):
             tiles = slice(side * SIDE, (side + 1) * SIDE)
             nc.sync.dma_start(out=dst[:, tiles, :], in_=src.rearrange("(m p) k -> p m k", p=P)[:, tiles, :])
@@ -82,8 +85,8 @@ def tile_lstmcelllayernorm_kernel(
         nc.vector.memset(w_scales[:, first_round].bitcast(I32), 0)
         nc.vector.memset(w_scales[:, second_round].bitcast(I32), 0)
 
-        def load_weight_scales(cols):
-            for quadrant in range(4):
+        def load_weight_scales(cols, quadrants):
+            for quadrant in quadrants:
                 for w, scales in enumerate((W_ih_scales, W_hh_scales)):
                     first = 32 * quadrant + 4 * GROUPS * w
                     nc.sync.dma_start(
@@ -112,11 +115,13 @@ def tile_lstmcelllayernorm_kernel(
         shift = keep.tile([P, HIDDEN], BF16, name="shift")
 
         with tc.manual_schedule():
-            load_side(x_sb, x, 0)
-            load_side(h_sb, h, 0)
-            load_weight_scales(first_round)
-            load_biases()
+            for m in range(SIDE):
+                load_tile(x_sb, x, m)
+                load_tile(h_sb, h, m)
+            load_weight_scales(first_round, (0, 1))
             load_weight_columns(GATE_I * HIDDEN, CHUNK // 2)
+            load_weight_scales(first_round, (2, 3))
+            load_biases()
             load_side(x_sb, x, 1)
             load_side(h_sb, h, 1)
             load_weight_columns(GATE_I * HIDDEN + CHUNK // 2, CHUNK // 2)
@@ -184,7 +189,7 @@ def tile_lstmcelllayernorm_kernel(
                     out=f_bias[:, half * CHUNK : (half + 1) * CHUNK], in_=summed[:].rearrange("p q n -> p (q n)")
                 )
 
-        def gate_half(gate, half, side, between=None):
+        def gate_half(gate, half, side, bias_in=None, between=None):
             rows = slice(side * SIDE_ROWS, (side + 1) * SIDE_ROWS)
             func = ACT.Tanh if gate == GATE_G else ACT.Sigmoid
             pieces = []
@@ -203,6 +208,8 @@ def tile_lstmcelllayernorm_kernel(
                             start=(kg == 0),
                             stop=(kg == K_GROUPS - 1),
                         )
+                if bias_in is not None and piece == 0:
+                    bias_in()
                 value = gates.tile([P, 2, SIDE_ROWS], F32, name="gate%d" % gate, bufs=6)
                 for s in range(2):
                     block = first_block + s
@@ -314,8 +321,7 @@ def tile_lstmcelllayernorm_kernel(
         with tc.manual_schedule(engines={mybir.EngineType.PE}):
             for m in range(SIDE):
                 quantise_batch_tile(m)
-            lay_out_bias()
-            first_i[0] = gate_half(GATE_I, 0, 0, between=second_side_in)
+            first_i[0] = gate_half(GATE_I, 0, 0, bias_in=lay_out_bias, between=second_side_in)
             lay_out_f_bias()
             first_i[1] = gate_half(GATE_I, 0, 1)
 

@@ -46,6 +46,8 @@ def tile_lstmcelllayernorm_kernel(
         psum_acc = stack.enter_context(tc.psum_pool(name="psum_acc", bufs=4))
         psum_flip = stack.enter_context(tc.psum_pool(name="psum_flip", bufs=4))
 
+        zeros = keep.tile([P, CHUNK], BF16, name="zeros")
+        nc.vector.memset(zeros[:], 0.0)
         warm = keep.tile([P, 1], F32, name="warm")
         nc.vector.memset(warm[:], 0.0)
         nc.scalar.activation(out=warm[:], in_=warm[:], func=ACT.Sigmoid)
@@ -59,12 +61,9 @@ def tile_lstmcelllayernorm_kernel(
         h_sb = keep.tile([P, BATCH_TILES, HIDDEN], BF16, name="h_sb")
         c_sb = keep.tile([P, BATCH_TILES, HIDDEN], BF16, name="c_sb")
 
-        def load_tile(dst, src, m):
-            nc.sync.dma_start(out=dst[:, m, :], in_=src[m * P : (m + 1) * P, :])
-
         def load_side(dst, src, side):
             tiles = slice(side * SIDE, (side + 1) * SIDE)
-            nc.sync.dma_start(out=dst[:, tiles, :], in_=src.rearrange("(m p) k -> p m k", p=P)[:, tiles, :])
+            nc.sync.dma_start(out=dst[:, tiles, :], in_=src.rearrange("(p m) k -> p m k", p=P)[:, tiles, :])
 
         w_words = keep.tile([P, K_GROUPS, 4 * HIDDEN], U32, name="w_words", align_bytes=256)
 
@@ -79,28 +78,19 @@ def tile_lstmcelllayernorm_kernel(
         def load_weight_chunk(gate, half):
             load_weight_columns(gate * HIDDEN + half * CHUNK, CHUNK)
 
-        w_scales = keep.tile([P, 4 * HIDDEN], U8, name="w_scales", align_bytes=256)
-        first_round = slice(GATE_I * HIDDEN, (GATE_I + 1) * HIDDEN)
-        second_round = slice((GATE_I + 1) * HIDDEN, 4 * HIDDEN)
-        nc.vector.memset(w_scales[:, first_round].bitcast(I32), 0)
-        nc.vector.memset(w_scales[:, second_round].bitcast(I32), 0)
+        w_scales = []
+        for w in range(2):
+            w_scales.append(keep.tile([P, 4 * HIDDEN], U8, name="w_scales%d" % w, align_bytes=256))
+        for w in range(2):
+            nc.vector.memset(w_scales[w][:].bitcast(I32), 0)
 
-        def load_weight_scales(cols, quadrants):
-            for quadrant in quadrants:
-                for w, scales in enumerate((W_ih_scales, W_hh_scales)):
-                    first = 32 * quadrant + 4 * GROUPS * w
-                    nc.sync.dma_start(
-                        out=w_scales[first : first + 4 * GROUPS, cols].bitcast(I32),
-                        in_=scales[:, 4 * quadrant : 4 * quadrant + 4, cols].bitcast(I32),
-                    )
-
-        def load_weight_scales_aside(cols):
-            for quadrant in range(4):
-                for w, scales in enumerate((W_ih_scales, W_hh_scales)):
-                    first = 32 * quadrant + 4 * GROUPS * w
+        def load_weight_scales():
+            for w, scales in enumerate((W_ih_scales, W_hh_scales)):
+                for quadrant in range(4):
+                    first = 32 * quadrant
                     nc.gpsimd.dma_start(
-                        out=w_scales[first : first + 4 * GROUPS, cols].bitcast(F32),
-                        in_=scales[:, 4 * quadrant : 4 * quadrant + 4, cols].bitcast(F32),
+                        out=w_scales[w][first : first + 4 * GROUPS, :].bitcast(F32),
+                        in_=scales[:, 4 * quadrant : 4 * quadrant + 4, :].bitcast(F32),
                     )
 
         N_BLOCKS = 4 * HIDDEN // P
@@ -115,17 +105,12 @@ def tile_lstmcelllayernorm_kernel(
         shift = keep.tile([P, HIDDEN], BF16, name="shift")
 
         with tc.manual_schedule():
-            for m in range(SIDE):
-                load_tile(x_sb, x, m)
-                load_tile(h_sb, h, m)
-            load_weight_scales(first_round, (0, 1))
-            load_weight_columns(GATE_I * HIDDEN, CHUNK // 2)
-            load_weight_scales(first_round, (2, 3))
+            load_weight_scales()
+            for side in range(SIDES):
+                load_side(x_sb, x, side)
+                load_side(h_sb, h, side)
             load_biases()
-            load_side(x_sb, x, 1)
-            load_side(h_sb, h, 1)
-            load_weight_columns(GATE_I * HIDDEN + CHUNK // 2, CHUNK // 2)
-            load_weight_scales_aside(second_round)
+            load_weight_chunk(GATE_I, 0)
             load_weight_chunk(GATE_G, 0)
             load_weight_chunk(GATE_F, 0)
             load_weight_chunk(GATE_I, 1)
@@ -154,7 +139,7 @@ def tile_lstmcelllayernorm_kernel(
                             ident[:],
                         )
                 grouped = stage.tile([P, GROUPS, P, PACK], BF16, name="grouped", align_bytes=256)
-                if w == 1 and m < SIDE:
+                if w == 1:
                     nc.vector.tensor_copy(out=grouped[:].bitcast(F32), in_=flipped[:].rearrange("p g u r -> p g r u"))
                 else:
                     nc.scalar.copy(out=grouped[:].bitcast(F32), in_=flipped[:].rearrange("p g u r -> p g r u"))
@@ -172,13 +157,13 @@ def tile_lstmcelllayernorm_kernel(
         f_bias = keep.tile([P, HIDDEN], F32, name="f_bias")
 
         def lay_out_bias():
-            bias_sum = psum_acc.tile([P, N_BLOCKS], F32, name="bias_sum", tag="acc")
+            bias_sum = psum_flip.tile([P, N_BLOCKS], F32, name="bias_sum", tag="flip")
             nc.tensor.matmul(out=bias_sum[:], lhsT=bias_rows[:], rhs=pick[:], start=True, stop=True)
             nc.vector.tensor_copy(out=bias[:], in_=bias_sum[:])
 
         def lay_out_f_bias():
             for half in range(HALVES):
-                summed = psum_acc.tile([P, BLOCKS, P], F32, name="summed", tag="acc")
+                summed = psum_flip.tile([P, BLOCKS, P], F32, name="summed", tag="flip")
                 for q in range(BLOCKS):
                     block = GATE_F * (HIDDEN // P) + half * BLOCKS + q
                     nc.tensor.matmul(
@@ -189,7 +174,7 @@ def tile_lstmcelllayernorm_kernel(
                     out=f_bias[:, half * CHUNK : (half + 1) * CHUNK], in_=summed[:].rearrange("p q n -> p (q n)")
                 )
 
-        def gate_half(gate, half, side, bias_in=None, between=None):
+        def gate_half(gate, half, side):
             rows = slice(side * SIDE_ROWS, (side + 1) * SIDE_ROWS)
             func = ACT.Tanh if gate == GATE_G else ACT.Sigmoid
             pieces = []
@@ -202,21 +187,52 @@ def tile_lstmcelllayernorm_kernel(
                         nc.tensor.matmul_mx(
                             out=acc[:, s, :],
                             lhsT=w_words[:, kg, cols].bitcast(FP8X4),
-                            lhsT_scale=w_scales[4 * kg : P, cols],
+                            lhsT_scale=w_scales[kg // GROUPS][4 * (kg % GROUPS) : P, cols],
                             rhs=xh_codes[:, kg, rows].bitcast(FP8X4),
                             rhs_scale=xh_scales[:, kg, rows],
                             start=(kg == 0),
                             stop=(kg == K_GROUPS - 1),
                         )
-                if bias_in is not None and piece == 0:
-                    bias_in()
                 value = gates.tile([P, 2, SIDE_ROWS], F32, name="gate%d" % gate, bufs=6)
                 for s in range(2):
                     block = first_block + s
                     nc.scalar.activation(out=value[:, s, :], in_=acc[:, s, :], func=func, bias=bias[:, block : block + 1])
                 pieces.append(value)
-                if between is not None and piece == 0:
-                    between()
+            return pieces
+
+        def first_gate_half():
+            accs = []
+            for block in range(BLOCKS):
+                acc = psum_acc.tile([P, BATCH], F32, name="acc_first", tag="acc")
+                accs.append(acc)
+            for w in range(2):
+                for block in range(BLOCKS):
+                    cols = slice(block * P, (block + 1) * P)
+                    for kg in range(GROUPS * w, GROUPS * (w + 1)):
+                        nc.tensor.matmul_mx(
+                            out=accs[block][:],
+                            lhsT=w_words[:, kg, cols].bitcast(FP8X4),
+                            lhsT_scale=w_scales[w][4 * (kg % GROUPS) : P, cols],
+                            rhs=xh_codes[:, kg, :].bitcast(FP8X4),
+                            rhs_scale=xh_scales[:, kg, :],
+                            start=(kg == 0),
+                            stop=(kg == K_GROUPS - 1),
+                        )
+            pieces = {}
+            for side in range(SIDES):
+                pieces[side] = []
+            for piece in range(BLOCKS // 2):
+                for side in range(SIDES):
+                    value = gates.tile([P, 2, SIDE_ROWS], F32, name="gate%d" % GATE_I, bufs=6)
+                    pieces[side].append(value)
+                for s in range(2):
+                    block = 2 * piece + s
+                    for side in range(SIDES):
+                        nc.scalar.activation(
+                            out=pieces[side][piece][:, s, :],
+                            in_=accs[block][:, side * SIDE_ROWS : (side + 1) * SIDE_ROWS],
+                            func=ACT.Sigmoid, bias=bias[:, block : block + 1],
+                        )
             return pieces
 
         def to_rows(pieces):
@@ -227,6 +243,9 @@ def tile_lstmcelllayernorm_kernel(
                     nc.tensor.transpose(bank[:, q, :], pieces[q // 2][:, q % 2, t * P : (t + 1) * P], ident[:])
                 banks.append(bank[:].rearrange("p q j -> p (q j)"))
             return banks
+
+        def rows_of(out, m):
+            return out.rearrange("(p m) k -> p m k", p=P)[:, m, :]
 
         ig_T = {}
         o_T = {}
@@ -248,7 +267,7 @@ def tile_lstmcelllayernorm_kernel(
                         lhsT=xh_codes[:, kg, rows].bitcast(FP8X4),
                         lhsT_scale=xh_scales[:, kg, rows],
                         rhs=w_words[:, kg, w_cols].bitcast(FP8X4),
-                        rhs_scale=w_scales[4 * kg : P, w_cols],
+                        rhs_scale=w_scales[kg // GROUPS][4 * (kg % GROUPS) : P, w_cols],
                         start=(kg == 0),
                         stop=(kg == K_GROUPS - 1),
                     )
@@ -303,7 +322,7 @@ def tile_lstmcelllayernorm_kernel(
                     out=c_t[m][:, cols], in0=c_t[m][:, cols], scalar=rstd[m][:], in1=shift[:, cols],
                     op0=ALU.mult, op1=ALU.add,
                 )
-                nc.sync.dma_start(out=out_1[m * P : (m + 1) * P, cols], in_=c_t[m][:, cols])
+                nc.sync.dma_start(out=rows_of(out_1, m)[:, cols], in_=c_t[m][:, cols])
                 nc.scalar.activation(out=tanh_c[m][:, cols], in_=c_t[m][:, cols], func=ACT.Tanh)
 
         def output(half, side):
@@ -311,19 +330,23 @@ def tile_lstmcelllayernorm_kernel(
             o_rows = to_rows(o_T[(half, side)])
             for t, m in enumerate(range(side * SIDE, (side + 1) * SIDE)):
                 nc.vector.tensor_tensor(out=tanh_c[m][:, cols], in0=o_rows[t], in1=tanh_c[m][:, cols], op=ALU.mult)
-                nc.sync.dma_start(out=out_0[m * P : (m + 1) * P, cols], in_=tanh_c[m][:, cols])
+                nc.sync.dma_start(out=rows_of(out_0, m)[:, cols], in_=tanh_c[m][:, cols])
 
-        def second_side_in():
-            for m in range(SIDE, BATCH_TILES):
-                quantise_batch_tile(m)
+        def keep_clock_up(count):
+            idle = psum_acc.tile([P, CHUNK], F32, name="idle", tag="acc")
+            for n in range(count):
+                nc.tensor.matmul(out=idle[:], lhsT=zeros[:, 0:P], rhs=zeros[:], start=True, stop=True)
 
-        first_i = {}
         with tc.manual_schedule(engines={mybir.EngineType.PE}):
+            keep_clock_up(5)
             for m in range(SIDE):
                 quantise_batch_tile(m)
-            first_i[0] = gate_half(GATE_I, 0, 0, bias_in=lay_out_bias, between=second_side_in)
+            keep_clock_up(2)
+            for m in range(SIDE, BATCH_TILES):
+                quantise_batch_tile(m)
+            lay_out_bias()
             lay_out_f_bias()
-            first_i[1] = gate_half(GATE_I, 0, 1)
+            first_i = first_gate_half()
 
         cell_steps = [(0, (0, 1)), (1, (0,)), (1, (1,))]
         previous = None

@@ -67,31 +67,46 @@ def tile_lstmcelllayernorm_kernel(
 
         w_words = keep.tile([P, K_GROUPS, 4 * HIDDEN], U32, name="w_words", align_bytes=256)
 
-        def load_weight_columns(col0, width):
-            for w, words in enumerate((W_ih_words, W_hh_words)):
-                by_partition = words.rearrange("g p n t -> p g (n t)")
-                nc.sync.dma_start(
-                    out=w_words[:, GROUPS * w : GROUPS * (w + 1), col0 : col0 + width].bitcast(I32),
-                    in_=by_partition[:, :, PACK * col0 : PACK * (col0 + width)].bitcast(I32),
-                )
+        def load_weight(w, gate, half):
+            col0 = gate * HIDDEN + half * CHUNK
+            by_partition = (W_ih_words, W_hh_words)[w].rearrange("g p n t -> p g (n t)")
+            nc.sync.dma_start(
+                out=w_words[:, GROUPS * w : GROUPS * (w + 1), col0 : col0 + CHUNK].bitcast(I32),
+                in_=by_partition[:, :, PACK * col0 : PACK * (col0 + CHUNK)].bitcast(I32),
+            )
 
         def load_weight_chunk(gate, half):
-            load_weight_columns(gate * HIDDEN + half * CHUNK, CHUNK)
+            for w in range(2):
+                load_weight(w, gate, half)
 
         w_scales = []
         for w in range(2):
             w_scales.append(keep.tile([P, 4 * HIDDEN], U8, name="w_scales%d" % w, align_bytes=256))
-        for w in range(2):
-            nc.vector.memset(w_scales[w][:].bitcast(I32), 0)
+        first_chunk = slice(0, CHUNK)
+        sync_rest = slice(CHUNK, GATE_F * HIDDEN + CHUNK)
+        aside_first = slice(GATE_G * HIDDEN, 4 * HIDDEN)
+        aside_rest = slice(GATE_F * HIDDEN + CHUNK, GATE_G * HIDDEN)
+        for cols in (first_chunk, aside_first, sync_rest, aside_rest):
+            for w in range(2):
+                nc.vector.memset(w_scales[w][:, cols].bitcast(I32), 0)
 
-        def load_weight_scales():
-            for w, scales in enumerate((W_ih_scales, W_hh_scales)):
-                for quadrant in range(4):
-                    first = 32 * quadrant
-                    nc.gpsimd.dma_start(
-                        out=w_scales[w][first : first + 4 * GROUPS, :].bitcast(F32),
-                        in_=scales[:, 4 * quadrant : 4 * quadrant + 4, :].bitcast(F32),
-                    )
+        SCALES = (W_ih_scales, W_hh_scales)
+
+        def load_scales(w, cols):
+            for quadrant in range(4):
+                first = 32 * quadrant
+                nc.sync.dma_start(
+                    out=w_scales[w][first : first + 4 * GROUPS, cols].bitcast(I32),
+                    in_=SCALES[w][:, 4 * quadrant : 4 * quadrant + 4, cols].bitcast(I32),
+                )
+
+        def load_scales_aside(w, cols):
+            for quadrant in range(4):
+                first = 32 * quadrant
+                nc.gpsimd.dma_start(
+                    out=w_scales[w][first : first + 4 * GROUPS, cols].bitcast(F32),
+                    in_=SCALES[w][:, 4 * quadrant : 4 * quadrant + 4, cols].bitcast(F32),
+                )
 
         N_BLOCKS = 4 * HIDDEN // P
         bias_rows = keep.tile([P, P], BF16, name="bias_rows")
@@ -105,13 +120,20 @@ def tile_lstmcelllayernorm_kernel(
         shift = keep.tile([P, HIDDEN], BF16, name="shift")
 
         with tc.manual_schedule():
-            load_weight_scales()
+            for cols in (aside_first, aside_rest):
+                for w in range(2):
+                    load_scales_aside(w, cols)
             for side in range(SIDES):
                 load_side(x_sb, x, side)
                 load_side(h_sb, h, side)
+            load_scales(0, first_chunk)
+            load_weight(0, GATE_I, 0)
+            load_scales(1, first_chunk)
+            load_weight(1, GATE_I, 0)
             load_biases()
-            load_weight_chunk(GATE_I, 0)
             load_weight_chunk(GATE_G, 0)
+            for w in range(2):
+                load_scales(w, sync_rest)
             load_weight_chunk(GATE_F, 0)
             load_weight_chunk(GATE_I, 1)
             for side in range(SIDES):
@@ -126,30 +148,30 @@ def tile_lstmcelllayernorm_kernel(
         xh_codes = keep.tile([P, K_GROUPS, BATCH], U32, name="xh_codes", align_bytes=256)
         xh_scales = keep.tile([P, K_GROUPS, BATCH], U8, name="xh_scales", align_bytes=256)
 
-        def quantise_batch_tile(m):
+        def quantise(w, m):
             per_group = HIDDEN // 2 // GROUPS
-            for w, src in enumerate((x_sb, h_sb)):
-                words = src[:, m, :].bitcast(F32)
-                flipped = psum_flip.tile([P, GROUPS, 2, P], F32, name="flipped", tag="flip")
-                for g in range(GROUPS):
-                    for u in range(2):
-                        nc.tensor.transpose(
-                            flipped[:, g, u, :],
-                            words[:, per_group * g + u : per_group * (g + 1) : 2],
-                            ident[:],
-                        )
-                grouped = stage.tile([P, GROUPS, P, PACK], BF16, name="grouped", align_bytes=256)
-                if w == 1:
-                    nc.vector.tensor_copy(out=grouped[:].bitcast(F32), in_=flipped[:].rearrange("p g u r -> p g r u"))
-                else:
-                    nc.scalar.copy(out=grouped[:].bitcast(F32), in_=flipped[:].rearrange("p g u r -> p g r u"))
-                for g in range(GROUPS):
-                    kg = GROUPS * w + g
-                    nc.vector.quantize_mx(
-                        out=xh_codes[:, kg, m * P : (m + 1) * P].bitcast(FP8X4),
-                        scales=xh_scales[:, kg, m * P : (m + 1) * P],
-                        in_=grouped[:, g, :, :].rearrange("p r t -> p (r t)"),
+            src = (x_sb, h_sb)[w]
+            words = src[:, m, :].bitcast(F32)
+            flipped = psum_flip.tile([P, GROUPS, 2, P], F32, name="flipped", tag="flip")
+            for g in range(GROUPS):
+                for u in range(2):
+                    nc.tensor.transpose(
+                        flipped[:, g, u, :],
+                        words[:, per_group * g + u : per_group * (g + 1) : 2],
+                        ident[:],
                     )
+            grouped = stage.tile([P, GROUPS, P, PACK], BF16, name="grouped", align_bytes=256)
+            if w == 1:
+                nc.vector.tensor_copy(out=grouped[:].bitcast(F32), in_=flipped[:].rearrange("p g u r -> p g r u"))
+            else:
+                nc.scalar.copy(out=grouped[:].bitcast(F32), in_=flipped[:].rearrange("p g u r -> p g r u"))
+            for g in range(GROUPS):
+                kg = GROUPS * w + g
+                nc.vector.quantize_mx(
+                    out=xh_codes[:, kg, m * P : (m + 1) * P].bitcast(FP8X4),
+                    scales=xh_scales[:, kg, m * P : (m + 1) * P],
+                    in_=grouped[:, g, :, :].rearrange("p r t -> p (r t)"),
+                )
 
         pick = keep.tile([P, N_BLOCKS], BF16, name="pick")
         nc.vector.tensor_tensor(out=pick[:], in0=ident[:, 0:N_BLOCKS], in1=ident[:, N_BLOCKS : 2 * N_BLOCKS], op=ALU.add)
@@ -174,7 +196,7 @@ def tile_lstmcelllayernorm_kernel(
                     out=f_bias[:, half * CHUNK : (half + 1) * CHUNK], in_=summed[:].rearrange("p q n -> p (q n)")
                 )
 
-        def gate_half(gate, half, side):
+        def gate_half(gate, half, side, between=None):
             rows = slice(side * SIDE_ROWS, (side + 1) * SIDE_ROWS)
             func = ACT.Tanh if gate == GATE_G else ACT.Sigmoid
             pieces = []
@@ -198,16 +220,19 @@ def tile_lstmcelllayernorm_kernel(
                     block = first_block + s
                     nc.scalar.activation(out=value[:, s, :], in_=acc[:, s, :], func=func, bias=bias[:, block : block + 1])
                 pieces.append(value)
+                if between is not None and piece == 0:
+                    between()
             return pieces
 
-        def first_gate_half():
+        def gate_i_half(half, biases_in=None):
+            first_block = half * BLOCKS
             accs = []
             for block in range(BLOCKS):
                 acc = psum_acc.tile([P, BATCH], F32, name="acc_first", tag="acc")
                 accs.append(acc)
             for w in range(2):
                 for block in range(BLOCKS):
-                    cols = slice(block * P, (block + 1) * P)
+                    cols = slice((first_block + block) * P, (first_block + block + 1) * P)
                     for kg in range(GROUPS * w, GROUPS * (w + 1)):
                         nc.tensor.matmul_mx(
                             out=accs[block][:],
@@ -218,12 +243,14 @@ def tile_lstmcelllayernorm_kernel(
                             start=(kg == 0),
                             stop=(kg == K_GROUPS - 1),
                         )
+                if biases_in is not None and w == 0:
+                    biases_in()
             pieces = {}
             for side in range(SIDES):
                 pieces[side] = []
             for piece in range(BLOCKS // 2):
                 for side in range(SIDES):
-                    value = gates.tile([P, 2, SIDE_ROWS], F32, name="gate%d" % GATE_I, bufs=6)
+                    value = gates.tile([P, 2, SIDE_ROWS], F32, name="gate0", bufs=6)
                     pieces[side].append(value)
                 for s in range(2):
                     block = 2 * piece + s
@@ -231,7 +258,7 @@ def tile_lstmcelllayernorm_kernel(
                         nc.scalar.activation(
                             out=pieces[side][piece][:, s, :],
                             in_=accs[block][:, side * SIDE_ROWS : (side + 1) * SIDE_ROWS],
-                            func=ACT.Sigmoid, bias=bias[:, block : block + 1],
+                            func=ACT.Sigmoid, bias=bias[:, first_block + block : first_block + block + 1],
                         )
             return pieces
 
@@ -271,7 +298,7 @@ def tile_lstmcelllayernorm_kernel(
                         start=(kg == 0),
                         stop=(kg == K_GROUPS - 1),
                     )
-                f = gates.tile([P, CHUNK], F32, name="f")
+                f = gates.tile([P, CHUNK], F32, name="f", bufs=4)
                 nc.vector.tensor_tensor(out=f[:], in0=acc[:], in1=f_bias[:, cols], op=ALU.add)
                 nc.scalar.activation(out=f[:], in_=f[:], func=ACT.Sigmoid)
                 if half == 0:
@@ -337,16 +364,20 @@ def tile_lstmcelllayernorm_kernel(
             for n in range(count):
                 nc.tensor.matmul(out=idle[:], lhsT=zeros[:, 0:P], rhs=zeros[:], start=True, stop=True)
 
-        with tc.manual_schedule(engines={mybir.EngineType.PE}):
-            keep_clock_up(5)
-            for m in range(SIDE):
-                quantise_batch_tile(m)
-            keep_clock_up(2)
-            for m in range(SIDE, BATCH_TILES):
-                quantise_batch_tile(m)
+        def lay_out_biases():
             lay_out_bias()
             lay_out_f_bias()
-            first_i = first_gate_half()
+
+        with tc.manual_schedule(engines={mybir.EngineType.PE}):
+            keep_clock_up(5)
+            for w in range(2):
+                for m in range(SIDE):
+                    quantise(w, m)
+            keep_clock_up(2)
+            for w in range(2):
+                for m in range(SIDE, BATCH_TILES):
+                    quantise(w, m)
+            first_i = gate_i_half(0, biases_in=lay_out_biases)
 
         cell_steps = [(0, (0, 1)), (1, (0,)), (1, (1,))]
         previous = None

@@ -161,10 +161,7 @@ def tile_lstmcelllayernorm_kernel(
                         ident[:],
                     )
             grouped = stage.tile([P, GROUPS, P, PACK], BF16, name="grouped", align_bytes=256)
-            if w == 1:
-                nc.vector.tensor_copy(out=grouped[:].bitcast(F32), in_=flipped[:].rearrange("p g u r -> p g r u"))
-            else:
-                nc.scalar.copy(out=grouped[:].bitcast(F32), in_=flipped[:].rearrange("p g u r -> p g r u"))
+            nc.scalar.copy(out=grouped[:].bitcast(F32), in_=flipped[:].rearrange("p g u r -> p g r u"))
             for g in range(GROUPS):
                 kg = GROUPS * w + g
                 nc.vector.quantize_mx(

from contextlib import ExitStack

import concourse.mybir as mybir
from concourse.masks import make_identity

F32 = mybir.dt.float32
BF16 = mybir.dt.bfloat16
I32 = mybir.dt.int32
U32 = mybir.dt.uint32
U8 = mybir.dt.uint8
FP8X4 = mybir.dt.float8_e4m3fn_x4
ALU = mybir.AluOpType
ACT = mybir.ActivationFunctionType

P = 128
PACK = 4
BATCH = 512
HIDDEN = 1024
BATCH_TILES = BATCH // P
GROUPS = HIDDEN // (P * PACK)
K_GROUPS = 2 * GROUPS
CHUNK = 512
HALVES = HIDDEN // CHUNK
BLOCKS = CHUNK // P
SIDE = 2
SIDE_ROWS = SIDE * P
SIDES = BATCH_TILES // SIDE
EPS = 1e-5

GATE_I, GATE_F, GATE_O, GATE_G = 0, 1, 2, 3
CELL_GATES = (GATE_I, GATE_G, GATE_F)

FLOPS = 2 * BATCH * (2 * HIDDEN) * (4 * HIDDEN)


def tile_lstmcelllayernorm_kernel(
    tc, x, h, c, W_ih_words, W_ih_scales, b_ih, W_hh_words, W_hh_scales, b_hh, ln_w, ln_b, out_0, out_1
):
    nc = tc.nc
    with ExitStack() as stack:
        keep = stack.enter_context(tc.tile_pool(name="keep", bufs=1))
        stage = stack.enter_context(tc.tile_pool(name="stage", bufs=4))
        gates = stack.enter_context(tc.tile_pool(name="gates", bufs=4))
        work = stack.enter_context(tc.tile_pool(name="work", bufs=2))
        stats = stack.enter_context(tc.tile_pool(name="stats", bufs=4))
        psum_acc = stack.enter_context(tc.psum_pool(name="psum_acc", bufs=4))
        psum_flip = stack.enter_context(tc.psum_pool(name="psum_flip", bufs=4))

        zeros = keep.tile([P, CHUNK], BF16, name="zeros")
        nc.vector.memset(zeros[:], 0.0)
        warm = keep.tile([P, 1], F32, name="warm")
        nc.vector.memset(warm[:], 0.0)
        nc.scalar.activation(out=warm[:], in_=warm[:], func=ACT.Sigmoid)

        ident = keep.tile([P, P], F32, name="ident")
        make_identity(nc, ident[:])
        neg_half = keep.tile([P, 1], F32, name="neg_half")
        nc.gpsimd.memset(neg_half[:], -0.5)

        x_sb = keep.tile([P, BATCH_TILES, HIDDEN], BF16, name="x_sb")
        h_sb = keep.tile([P, BATCH_TILES, HIDDEN], BF16, name="h_sb")
        c_sb = keep.tile([P, BATCH_TILES, HIDDEN], BF16, name="c_sb")

        def load_side(dst, src, side):
            tiles = slice(side * SIDE, (side + 1) * SIDE)
            nc.sync.dma_start(out=dst[:, tiles, :], in_=src.rearrange("(p m) k -> p m k", p=P)[:, tiles, :])

        w_words = keep.tile([P, K_GROUPS, 4 * HIDDEN], U32, name="w_words", align_bytes=256)

        def load_weight(w, gate, half):
            col0 = gate * HIDDEN + half * CHUNK
            by_partition = (W_ih_words, W_hh_words)[w].rearrange("g p n t -> p g (n t)")
            nc.sync.dma_start(
                out=w_words[:, GROUPS * w : GROUPS * (w + 1), col0 : col0 + CHUNK].bitcast(I32),
                in_=by_partition[:, :, PACK * col0 : PACK * (col0 + CHUNK)].bitcast(I32),
            )

        def load_weight_chunk(gate, half):
            for w in range(2):
                load_weight(w, gate, half)

        w_scales = []
        for w in range(2):
            w_scales.append(keep.tile([P, 4 * HIDDEN], U8, name="w_scales%d" % w, align_bytes=256))
        first_chunk = slice(0, CHUNK)
        sync_rest = slice(CHUNK, GATE_F * HIDDEN + CHUNK)
        aside_first = slice(GATE_G * HIDDEN, 4 * HIDDEN)
        aside_rest = slice(GATE_F * HIDDEN + CHUNK, GATE_G * HIDDEN)
        for cols in (first_chunk, aside_first, sync_rest, aside_rest):
            for w in range(2):
                nc.vector.memset(w_scales[w][:, cols].bitcast(I32), 0)

        SCALES = (W_ih_scales, W_hh_scales)

        def load_scales(w, cols):
            for quadrant in range(4):
                first = 32 * quadrant
                nc.sync.dma_start(
                    out=w_scales[w][first : first + 4 * GROUPS, cols].bitcast(I32),
                    in_=SCALES[w][:, 4 * quadrant : 4 * quadrant + 4, cols].bitcast(I32),
                )

        def load_scales_aside(w, cols):
            for quadrant in range(4):
                first = 32 * quadrant
                nc.gpsimd.dma_start(
                    out=w_scales[w][first : first + 4 * GROUPS, cols].bitcast(F32),
                    in_=SCALES[w][:, 4 * quadrant : 4 * quadrant + 4, cols].bitcast(F32),
                )

        N_BLOCKS = 4 * HIDDEN // P
        bias_rows = keep.tile([P, P], BF16, name="bias_rows")
        nc.vector.memset(bias_rows[:], 0.0)

        def load_biases():
            nc.sync.dma_start(out=bias_rows[0:N_BLOCKS, :], in_=b_ih.rearrange("(r n) -> r n", n=P))
            nc.sync.dma_start(out=bias_rows[N_BLOCKS : 2 * N_BLOCKS, :], in_=b_hh.rearrange("(r n) -> r n", n=P))

        gain = keep.tile([P, HIDDEN], BF16, name="gain")
        shift = keep.tile([P, HIDDEN], BF16, name="shift")

        with tc.manual_schedule():
            for cols in (aside_first, aside_rest):
                for w in range(2):
                    load_scales_aside(w, cols)
            for side in range(SIDES):
                load_side(x_sb, x, side)
                load_side(h_sb, h, side)
            load_scales(0, first_chunk)
            load_weight(0, GATE_I, 0)
            load_scales(1, first_chunk)
            load_weight(1, GATE_I, 0)
            load_biases()
            load_weight_chunk(GATE_G, 0)
            for w in range(2):
                load_scales(w, sync_rest)
            load_weight_chunk(GATE_F, 0)
            load_weight_chunk(GATE_I, 1)
            for side in range(SIDES):
                load_side(c_sb, c, side)
            load_weight_chunk(GATE_G, 1)
            load_weight_chunk(GATE_F, 1)
            for half in range(HALVES):
                load_weight_chunk(GATE_O, half)
            nc.sync.dma_start(out=gain[:], in_=ln_w.partition_broadcast(P))
            nc.sync.dma_start(out=shift[:], in_=ln_b.partition_broadcast(P))

        xh_codes = keep.tile([P, K_GROUPS, BATCH], U32, name="xh_codes", align_bytes=256)
        xh_scales = keep.tile([P, K_GROUPS, BATCH], U8, name="xh_scales", align_bytes=256)

        def quantise(w, m):
            per_group = HIDDEN // 2 // GROUPS
            src = (x_sb, h_sb)[w]
            words = src[:, m, :].bitcast(F32)
            flipped = psum_flip.tile([P, GROUPS, 2, P], F32, name="flipped", tag="flip")
            for g in range(GROUPS):
                for u in range(2):
                    nc.tensor.transpose(
                        flipped[:, g, u, :],
                        words[:, per_group * g + u : per_group * (g + 1) : 2],
                        ident[:],
                    )
            grouped = stage.tile([P, GROUPS, P, PACK], BF16, name="grouped", align_bytes=256)
            nc.scalar.copy(out=grouped[:].bitcast(F32), in_=flipped[:].rearrange("p g u r -> p g r u"))
            for g in range(GROUPS):
                kg = GROUPS * w + g
                nc.vector.quantize_mx(
                    out=xh_codes[:, kg, m * P : (m + 1) * P].bitcast(FP8X4),
                    scales=xh_scales[:, kg, m * P : (m + 1) * P],
                    in_=grouped[:, g, :, :].rearrange("p r t -> p (r t)"),
                )

        pick = keep.tile([P, N_BLOCKS], BF16, name="pick")
        nc.vector.tensor_tensor(out=pick[:], in0=ident[:, 0:N_BLOCKS], in1=ident[:, N_BLOCKS : 2 * N_BLOCKS], op=ALU.add)
        bias = keep.tile([P, N_BLOCKS], F32, name="bias")
        f_bias = keep.tile([P, HIDDEN], F32, name="f_bias")

        def lay_out_bias():
            bias_sum = psum_flip.tile([P, N_BLOCKS], F32, name="bias_sum", tag="flip")
            nc.tensor.matmul(out=bias_sum[:], lhsT=bias_rows[:], rhs=pick[:], start=True, stop=True)
            nc.vector.tensor_copy(out=bias[:], in_=bias_sum[:])

        def lay_out_f_bias():
            for half in range(HALVES):
                summed = psum_flip.tile([P, BLOCKS, P], F32, name="summed", tag="flip")
                for q in range(BLOCKS):
                    block = GATE_F * (HIDDEN // P) + half * BLOCKS + q
                    nc.tensor.matmul(
                        out=summed[:, q, :], lhsT=pick[:, block : block + 1].to_broadcast([P, P]), rhs=bias_rows[:],
                        start=True, stop=True,
                    )
                nc.vector.tensor_copy(
                    out=f_bias[:, half * CHUNK : (half + 1) * CHUNK], in_=summed[:].rearrange("p q n -> p (q n)")
                )

        def gate_half(gate, half, side, between=None):
            rows = slice(side * SIDE_ROWS, (side + 1) * SIDE_ROWS)
            func = ACT.Tanh if gate == GATE_G else ACT.Sigmoid
            pieces = []
            for piece in range(BLOCKS // 2):
                acc = psum_acc.tile([P, 2, SIDE_ROWS], F32, name="acc", tag="acc")
                first_block = gate * (HIDDEN // P) + half * BLOCKS + 2 * piece
                for s in range(2):
                    cols = slice((first_block + s) * P, (first_block + s + 1) * P)
                    for kg in range(K_GROUPS):
                        nc.tensor.matmul_mx(
                            out=acc[:, s, :],
                            lhsT=w_words[:, kg, cols].bitcast(FP8X4),
                            lhsT_scale=w_scales[kg // GROUPS][4 * (kg % GROUPS) : P, cols],
                            rhs=xh_codes[:, kg, rows].bitcast(FP8X4),
                            rhs_scale=xh_scales[:, kg, rows],
                            start=(kg == 0),
                            stop=(kg == K_GROUPS - 1),
                        )
                value = gates.tile([P, 2, SIDE_ROWS], F32, name="gate%d" % gate, bufs=6)
                for s in range(2):
                    block = first_block + s
                    nc.scalar.activation(out=value[:, s, :], in_=acc[:, s, :], func=func, bias=bias[:, block : block + 1])
                pieces.append(value)
                if between is not None and piece == 0:
                    between()
            return pieces

        def gate_i_half(half, biases_in=None):
            first_block = half * BLOCKS
            accs = []
            for block in range(BLOCKS):
                acc = psum_acc.tile([P, BATCH], F32, name="acc_first", tag="acc")
                accs.append(acc)
            for w in range(2):
                for block in range(BLOCKS):
                    cols = slice((first_block + block) * P, (first_block + block + 1) * P)
                    for kg in range(GROUPS * w, GROUPS * (w + 1)):
                        nc.tensor.matmul_mx(
                            out=accs[block][:],
                            lhsT=w_words[:, kg, cols].bitcast(FP8X4),
                            lhsT_scale=w_scales[w][4 * (kg % GROUPS) : P, cols],
                            rhs=xh_codes[:, kg, :].bitcast(FP8X4),
                            rhs_scale=xh_scales[:, kg, :],
                            start=(kg == 0),
                            stop=(kg == K_GROUPS - 1),
                        )
                if biases_in is not None and w == 0:
                    biases_in()
            pieces = {}
            for side in range(SIDES):
                pieces[side] = []
            for piece in range(BLOCKS // 2):
                for side in range(SIDES):
                    value = gates.tile([P, 2, SIDE_ROWS], F32, name="gate0", bufs=6)
                    pieces[side].append(value)
                for s in range(2):
                    block = 2 * piece + s
                    for side in range(SIDES):
                        nc.scalar.activation(
                            out=pieces[side][piece][:, s, :],
                            in_=accs[block][:, side * SIDE_ROWS : (side + 1) * SIDE_ROWS],
                            func=ACT.Sigmoid, bias=bias[:, first_block + block : first_block + block + 1],
                        )
            return pieces

        def to_rows(pieces):
            banks = []
            for t in range(SIDE):
                bank = psum_flip.tile([P, BLOCKS, P], F32, name="bank", tag="flip")
                for q in range(BLOCKS):
                    nc.tensor.transpose(bank[:, q, :], pieces[q // 2][:, q % 2, t * P : (t + 1) * P], ident[:])
                banks.append(bank[:].rearrange("p q j -> p (q j)"))
            return banks

        def rows_of(out, m):
            return out.rearrange("(p m) k -> p m k", p=P)[:, m, :]

        ig_T = {}
        o_T = {}
        u = {}
        u_sum = {}
        c_t = {}
        rstd = {}
        tanh_c = {}

        def forget_times_c(half, side):
            cols = slice(half * CHUNK, (half + 1) * CHUNK)
            w_cols = slice(GATE_F * HIDDEN + half * CHUNK, GATE_F * HIDDEN + (half + 1) * CHUNK)
            for m in range(side * SIDE, (side + 1) * SIDE):
                rows = slice(m * P, (m + 1) * P)
                acc = psum_acc.tile([P, CHUNK], F32, name="acc_rows", tag="acc")
                for kg in range(K_GROUPS):
                    nc.tensor.matmul_mx(
                        out=acc[:],
                        lhsT=xh_codes[:, kg, rows].bitcast(FP8X4),
                        lhsT_scale=xh_scales[:, kg, rows],
                        rhs=w_words[:, kg, w_cols].bitcast(FP8X4),
                        rhs_scale=w_scales[kg // GROUPS][4 * (kg % GROUPS) : P, w_cols],
                        start=(kg == 0),
                        stop=(kg == K_GROUPS - 1),
                    )
                f = gates.tile([P, CHUNK], F32, name="f", bufs=4)
                nc.vector.tensor_tensor(out=f[:], in0=acc[:], in1=f_bias[:, cols], op=ALU.add)
                nc.scalar.activation(out=f[:], in_=f[:], func=ACT.Sigmoid)
                if half == 0:
                    u[m] = work.tile([P, HIDDEN], F32, name="u", bufs=BATCH_TILES)
                    u_sum[m] = stats.tile([P, HALVES], F32, name="u_sum")
                nc.vector.tensor_tensor(out=u[m][:, cols], in0=f[:], in1=c_sb[:, m, cols], op=ALU.mult)

        def add_products(half, side):
            cols = slice(half * CHUNK, (half + 1) * CHUNK)
            ig_rows = to_rows(ig_T[(half, side)])
            tiles = range(side * SIDE, (side + 1) * SIDE)
            for t, m in enumerate(tiles):
                nc.vector.scalar_tensor_tensor(
                    out=u[m][:, cols], in0=ig_rows[t], scalar=1.0, in1=u[m][:, cols],
                    op0=ALU.mult, op1=ALU.add, accum_out=u_sum[m][:, half : half + 1],
                )
            if half == HALVES - 1:
                for m in tiles:
                    start_norm(m)

        def start_norm(m):
            neg_mean = stats.tile([P, 1], F32, name="neg_mean")
            nc.vector.tensor_scalar(
                out=neg_mean[:], in0=u_sum[m][:, 0:1], scalar1=u_sum[m][:, 1:2], scalar2=-1.0 / HIDDEN,
                op0=ALU.add, op1=ALU.mult,
            )
            squares = work.tile([P, HIDDEN], BF16, name="squares")
            var = stats.tile([P, 1], F32, name="var")
            nc.scalar.activation(
                out=squares[:], in_=u[m][:], func=ACT.Square, bias=neg_mean[:], scale=1.0, accum_out=var[:]
            )
            c_t[m] = work.tile([P, HIDDEN], F32, name="c_t", bufs=3)
            nc.vector.scalar_tensor_tensor(
                out=c_t[m][:], in0=u[m][:], scalar=neg_mean[:], in1=gain[:], op0=ALU.add, op1=ALU.mult
            )
            var_eps = stats.tile([P, 1], F32, name="var_eps")
            nc.gpsimd.tensor_scalar(
                out=var_eps[:], in0=var[:], scalar1=1.0 / HIDDEN, scalar2=EPS, op0=ALU.mult, op1=ALU.add
            )
            rstd[m] = stats.tile([P, 1], F32, name="rstd")
            nc.gpsimd.tensor_tensor(out=rstd[m][:], in0=var_eps[:], in1=neg_half[:], op=ALU.pow)

        def finish_norm(m):
            tanh_c[m] = work.tile([P, HIDDEN], F32, name="tanh_c", bufs=BATCH_TILES)
            for half in range(HALVES):
                cols = slice(half * CHUNK, (half + 1) * CHUNK)
                nc.vector.scalar_tensor_tensor(
                    out=c_t[m][:, cols], in0=c_t[m][:, cols], scalar=rstd[m][:], in1=shift[:, cols],
                    op0=ALU.mult, op1=ALU.add,
                )
                nc.sync.dma_start(out=rows_of(out_1, m)[:, cols], in_=c_t[m][:, cols])
                nc.scalar.activation(out=tanh_c[m][:, cols], in_=c_t[m][:, cols], func=ACT.Tanh)

        def output(half, side):
            cols = slice(half * CHUNK, (half + 1) * CHUNK)
            o_rows = to_rows(o_T[(half, side)])
            for t, m in enumerate(range(side * SIDE, (side + 1) * SIDE)):
                nc.vector.tensor_tensor(out=tanh_c[m][:, cols], in0=o_rows[t], in1=tanh_c[m][:, cols], op=ALU.mult)
                nc.sync.dma_start(out=rows_of(out_0, m)[:, cols], in_=tanh_c[m][:, cols])

        def keep_clock_up(count):
            idle = psum_acc.tile([P, CHUNK], F32, name="idle", tag="acc")
            for n in range(count):
                nc.tensor.matmul(out=idle[:], lhsT=zeros[:, 0:P], rhs=zeros[:], start=True, stop=True)

        def lay_out_biases():
            lay_out_bias()
            lay_out_f_bias()

        with tc.manual_schedule(engines={mybir.EngineType.PE}):
            keep_clock_up(5)
            for w in range(2):
                for m in range(SIDE):
                    quantise(w, m)
            keep_clock_up(2)
            for w in range(2):
                for m in range(SIDE, BATCH_TILES):
                    quantise(w, m)
            first_i = gate_i_half(0, biases_in=lay_out_biases)

        cell_steps = [(0, (0, 1)), (1, (0,)), (1, (1,))]
        previous = None
        for half, sides in cell_steps:
            i_T = first_i
            if previous is not None:
                i_T = {}
                for side in sides:
                    i_T[side] = gate_half(GATE_I, half, side)
            if previous is not None:
                for side in previous[1]:
                    add_products(previous[0], side)
            for side in sides:
                g_T = gate_half(GATE_G, half, side)
                ig_T[(half, side)] = []
                for piece in range(BLOCKS // 2):
                    product = gates.tile([P, 2, SIDE_ROWS], F32, name="product", bufs=6)
                    nc.vector.tensor_tensor(out=product[:], in0=i_T[side][piece][:], in1=g_T[piece][:], op=ALU.mult)
                    ig_T[(half, side)].append(product)
            for side in sides:
                forget_times_c(half, side)
            if previous is not None and previous[0] == HALVES - 1:
                for side in previous[1]:
                    for m in range(side * SIDE, (side + 1) * SIDE):
                        finish_norm(m)
            previous = (half, sides)

        out_steps = [(half, side) for side in range(SIDES) for half in range(HALVES)]
        for position, (half, side) in enumerate(out_steps):
            o_T[(half, side)] = gate_half(GATE_O, half, side)
            if position == 0:
                add_products(HALVES - 1, SIDES - 1)
            else:
                output(*out_steps[position - 1])
            if position == 1:
                for m in range((SIDES - 1) * SIDE, SIDES * SIDE):
                    finish_norm(m)
        output(*out_steps[-1])
